import numpy as np
import ml_dtypes


def mxq(x, axis, fmt="e4m3"):
    dtype, down = {"e4m3": (ml_dtypes.float8_e4m3fn, 7), "e5m2": (ml_dtypes.float8_e5m2, 14)}[fmt]
    v = np.moveaxis(np.asarray(x, np.float32).astype(ml_dtypes.bfloat16).astype(np.float64), axis, -1)
    blocks = v.reshape(v.shape[:-1] + (-1, 32))
    amax = np.abs(blocks).max(-1, keepdims=True)
    byte = np.maximum(np.where(amax > 0, np.frexp(amax)[1] - 1 + 127, 0) - down, 1)
    scale = np.exp2(byte - 127.0)
    codes = (blocks / scale).astype(np.float32).astype(dtype).astype(np.float64)
    return np.moveaxis((codes * scale).reshape(v.shape), -1, axis)


WIDE = False


def mx_kscale(k):
    if not WIDE:
        return np.ones(k)
    levels = np.array([10, -10, 5, -5, 0])
    a = np.random.permutation(np.resize(levels, k // 512 * 4)).reshape(k // 512, 4)
    idx = np.arange(k)
    return np.exp2(a[idx // 512, idx % 128 // 32])


BF16 = ml_dtypes.bfloat16


def bf(x):
    return np.asarray(x, np.float32).astype(BF16)


def f64(x):
    return np.asarray(x).astype(np.float64)


E2M1 = np.array([0.0, 0.5, 1.0, 1.5, 2.0, 3.0, 4.0, 6.0, -0.0, -0.5, -1.0, -1.5, -2.0, -3.0, -4.0, -6.0])


def pack_weight(w, fmt):
    k, n = w.shape
    w = f64(bf(w)).reshape(k // 32, 32, n)
    amax = np.abs(w).max(1)
    if fmt == "e4m3":
        byte = np.frexp(amax)[1] - 1 + 127 - 7
    else:
        mant, ex = np.frexp(amax / 6.0)
        byte = np.where(mant > 0.5, ex, ex - 1) + 127
    byte = np.clip(np.where(amax > 0, byte, 1), 1, 254)
    scaled = (w * np.exp2(127.0 - byte)[:, None, :]).reshape(k, n).astype(np.float32)
    by_word = np.ascontiguousarray(scaled.reshape(k // 512, 128, 4, n).transpose(0, 1, 3, 2))
    if fmt == "e4m3":
        words = by_word.astype(ml_dtypes.float8_e4m3fn).view(np.uint8)
    else:
        c = by_word.astype(ml_dtypes.float4_e2m1fn).view(np.uint8) & 0xF
        words = c[..., 0::2] | (c[..., 1::2] << 4)
    return np.ascontiguousarray(words), np.ascontiguousarray(byte.astype(np.uint8).reshape(k // 512, 16, n))


def unpack_weight(words, scales, fmt):
    g, p, n, _ = words.shape
    if fmt == "e4m3":
        vals = np.ascontiguousarray(words).view(ml_dtypes.float8_e4m3fn).astype(np.float64)
    else:
        nib = np.empty((g, p, n, 4), np.uint8)
        nib[..., 0::2] = words & 0xF
        nib[..., 1::2] = words >> 4
        vals = E2M1[nib]
    vals = vals * np.repeat(np.exp2(scales.astype(np.float64) - 127.0), 8, axis=1)[..., None]
    return vals.transpose(0, 1, 3, 2).reshape(g * 512, n)


B, S, E, H, G, P, K3, K5, K7 = 2, 512, 1024, 16, 4, 3, 3, 5, 7
D = E // H
HK = H // G


def dwconv_causal(x, w, b):
    k = w.shape[1]
    xp = np.pad(x, ((0, 0), (0, 0), (k - 1, 0), (0, 0)))
    y = b
    for i in range(k):
        y = y + xp[:, :, i:i + S, :] * w[:, i]
    return y


def split_heads(t):
    return t.reshape(B, S, H, D).swapaxes(1, 2)


def tranception_mix(t, ws_bs):
    parts = [t[:, :HK]]
    for g, (w, b) in enumerate(ws_bs):
        parts.append(dwconv_causal(t[:, (g + 1) * HK:(g + 2) * HK], w, b))
    return np.concatenate(parts, axis=1)


def setup_inputs():
    s = mx_kscale(E)
    hidden_states = bf(np.random.standard_normal((B, S, E)) * s)
    words, scales = pack_weight(np.random.standard_normal((E, P * E)) / np.sqrt(E) / s[:, None], 'e4m3')
    inp = {'hidden_states': hidden_states,
           'c_attn_w_words': words,
           'c_attn_w_scales': scales,
           'c_attn_b': bf(np.random.standard_normal(P * E) * 0.3)}
    for pre in ('q', 'k', 'v'):
        for kern in (K3, K5, K7):
            inp[pre + 'w' + str(kern)] = bf(np.random.standard_normal((D, kern)) / kern)
            inp[pre + 'b' + str(kern)] = bf(np.random.standard_normal(D) * 0.2)
    return inp


def reference(hidden_states, c_attn_w_words, c_attn_w_scales, c_attn_b,
              qw3, qb3, qw5, qb5, qw7, qb7,
              kw3, kb3, kw5, kb5, kw7, kb7,
              vw3, vb3, vw5, vb5, vw7, vb7):
    qkv = (mxq(f64(hidden_states), 2, 'e4m3') @ unpack_weight(c_attn_w_words, c_attn_w_scales, 'e4m3')) + f64(c_attn_b)
    q, k, v = np.split(qkv, P, axis=-1)
    q, k, v = split_heads(q), split_heads(k), split_heads(v)
    q = tranception_mix(q, [(f64(qw3), f64(qb3)), (f64(qw5), f64(qb5)), (f64(qw7), f64(qb7))])
    k = tranception_mix(k, [(f64(kw3), f64(kb3)), (f64(kw5), f64(kb5)), (f64(kw7), f64(kb7))])
    v = tranception_mix(v, [(f64(vw3), f64(vb3)), (f64(vw5), f64(vb5)), (f64(vw7), f64(vb7))])
    return q, k, v

@@ -1,0 +1,333 @@
+import concourse.mybir as mybir
+from concourse.masks import make_identity
+
+F32 = mybir.dt.float32
+BF16 = mybir.dt.bfloat16
+U8 = mybir.dt.uint8
+U32 = mybir.dt.uint32
+I32 = mybir.dt.int32
+FP8X4 = mybir.dt.float8_e4m3fn_x4
+MULT = mybir.AluOpType.mult
+ADD = mybir.AluOpType.add
+IDENTITY = mybir.ActivationFunctionType.Identity
+
+P = 128
+B, S, E, H, D = 2, 512, 1024, 16, 64
+PROJ = 3
+K_PASS = 512
+PASSES = E // K_PASS
+TOKEN_TILES = B * S // P
+CONV_TAPS = (3, 5, 7)
+GROUP_FEATURES = E // 4
+HALVES = GROUP_FEATURES // P
+GROUP_HEADS = GROUP_FEATURES // D
+FEATURE_TILES = PROJ * E // P
+J = S // P
+SLOT = 16
+LAST = 8
+PAD = 8
+CONV_ORDER = (2, 1, 0)
+AHEAD = 3
+
+FLOPS = 2 * B * S * E * PROJ * E
+
+
+def tile_tranceptionblockattention_pa_kernel(
+    tc,
+    hidden_states, c_attn_w_words, c_attn_w_scales, c_attn_b,
+    qw3, qb3, qw5, qb5, qw7, qb7,
+    kw3, kb3, kw5, kb5, kw7, kb7,
+    vw3, vb3, vw5, vb5, vw7, vb7,
+    out_0, out_1, out_2,
+):
+    nc = tc.nc
+    conv_w = ((qw3, qw5, qw7), (kw3, kw5, kw7), (vw3, vw5, vw7))
+    conv_b = ((qb3, qb5, qb7), (kb3, kb5, kb7), (vb3, vb5, vb7))
+    outs = (out_0, out_1, out_2)
+
+    with tc.tile_pool(name="keep", bufs=1) as keep, \
+            tc.tile_pool(name="work", bufs=3) as work, \
+            tc.tile_pool(name="sums", bufs=AHEAD + 2) as sums, \
+            tc.psum_pool(name="x_banks", bufs=AHEAD * HALVES) as x_banks, \
+            tc.psum_pool(name="y_banks", bufs=HALVES) as y_banks, \
+            tc.manual_schedule():
+
+        ident = keep.tile([P, P], F32)
+        x_sb = keep.tile([P, TOKEN_TILES, E], BF16)
+        grouped = keep.tile([P, PASSES, B * S, 4], BF16, align_bytes=64)
+        x_codes = keep.tile([P, PASSES, B * S], U32, align_bytes=64)
+        x_planes = keep.tile([P, PASSES, B * S], U8, align_bytes=64)
+        w_codes = keep.tile([P, PASSES, PROJ * E], U32, align_bytes=64)
+        w_planes = keep.tile([P, PASSES, PROJ * E], U8, align_bytes=64)
+        b_rows_bf = keep.tile([P, P], BF16)
+        b_rows = keep.tile([P, P], F32)
+        b_attn = keep.tile([P, FEATURE_TILES], F32)
+        b_plain = keep.tile([P, PROJ, GROUP_FEATURES], BF16)
+        cst_bf = [keep.tile([P, 6, SLOT], BF16, name="cst_bf%d" % pr) for pr in range(PROJ)]
+        cst = [keep.tile([P, 6, SLOT], F32, name="cst%d" % pr) for pr in range(PROJ)]
+        csum = [keep.tile([P, 3, LAST], F32, name="csum%d" % pr) for pr in range(PROJ)]
+        bias = [keep.tile([P, 3, HALVES, LAST], F32, name="bias%d" % pr) for pr in range(PROJ)]
+        far_bias = [keep.tile([P, 3, HALVES], F32, name="far_bias%d" % pr) for pr in range(PROJ)]
+        far_ring = [keep.tile([P, HALVES, J, PAD + P], F32, name="far%d" % i) for i in range(AHEAD + 2)]
+
+        nc.vector.memset(cst_bf[0][:], 0.0)
+        nc.vector.memset(b_rows_bf[:], 0.0)
+        nc.vector.memset(w_planes[:].bitcast(I32), 0)
+        nc.vector.memset(cst_bf[1][:], 0.0)
+        nc.vector.memset(cst_bf[2][:], 0.0)
+        make_identity(nc, ident[:])
+        for far_tile in far_ring:
+            nc.gpsimd.memset(far_tile[:, :, :, 0:PAD], 0.0)
+
+        x_rows = hidden_states.flatten_outer_dims().rearrange("(t p) k -> p t k", p=P)
+
+        def load_conv_constants(queue, pr):
+            for gi in range(3):
+                taps = CONV_TAPS[gi]
+                queue.dma_start(
+                    out=cst_bf[pr][:, gi, LAST - taps:LAST],
+                    in_=conv_w[pr][gi].unsqueeze(0).to_broadcast([P // D, D, taps]),
+                )
+                queue.dma_start(
+                    out=cst_bf[pr][:, 3 + gi, 0:1],
+                    in_=conv_b[pr][gi].rearrange("(d o) -> d o", o=1).unsqueeze(0).to_broadcast([P // D, D, 1]),
+                )
+
+        def load_w(pr):
+            for g in range(PASSES):
+                nc.sync.dma_start(
+                    out=w_codes[:, g, pr * E:(pr + 1) * E].bitcast(I32),
+                    in_=c_attn_w_words[g].rearrange("p n t -> p (n t)")[:, pr * E * 4:(pr + 1) * E * 4].bitcast(I32),
+                )
+
+        nc.scalar.dma_start(out=b_rows_bf[0:FEATURE_TILES, :], in_=c_attn_b.rearrange("(f p) -> f p", p=P))
+        load_conv_constants(nc.scalar, 0)
+        for first_tile in range(0, TOKEN_TILES, 2):
+            nc.sync.dma_start(out=x_sb[:, first_tile:first_tile + 2, :], in_=x_rows[:, first_tile:first_tile + 2, :])
+        for quad in range(4):
+            nc.sync.dma_start(
+                out=w_planes[32 * quad:32 * quad + 4, :, :].bitcast(I32),
+                in_=c_attn_w_scales[:, 4 * quad:4 * quad + 4, :].rearrange("g r n -> r g n").bitcast(I32),
+            )
+        load_w(0)
+        for pr in range(PROJ):
+            nc.sync.dma_start(out=b_plain[:, pr, :], in_=c_attn_b[pr * E:pr * E + GROUP_FEATURES].partition_broadcast(P))
+        load_conv_constants(nc.sync, 1)
+        load_w(1)
+        load_conv_constants(nc.sync, 2)
+        load_w(2)
+
+        nc.vector.tensor_copy(out=b_rows[:], in_=b_rows_bf[:])
+        b_cols = x_banks.tile([P, S], F32, tag="x")
+        nc.tensor.transpose(b_cols[:, 0:P], b_rows[:], ident[:])
+        nc.vector.tensor_copy(out=b_attn[:], in_=b_cols[:, 0:FEATURE_TILES])
+
+        def tap(pr, gi, back):
+            return cst[pr][:, gi, LAST - 1 - back:LAST - back]
+
+        def prepare_constants(pr):
+            nc.gpsimd.tensor_copy(out=cst[pr][:], in_=cst_bf[pr][:])
+            nc.gpsimd.tensor_copy(out=csum[pr][:, :, 0:1], in_=cst[pr][:, 0:3, LAST - 1:LAST])
+            for s in range(1, LAST - 1):
+                nc.gpsimd.tensor_tensor(
+                    out=csum[pr][:, :, s:s + 1],
+                    in0=csum[pr][:, :, s - 1:s],
+                    in1=cst[pr][:, 0:3, LAST - 1 - s:LAST - s],
+                    op=ADD,
+                )
+            for gi in CONV_ORDER:
+                for half in range(HALVES):
+                    ft = (pr * E + (gi + 1) * GROUP_FEATURES) // P + half
+                    nc.gpsimd.tensor_scalar(
+                        out=bias[pr][:, gi, half, 0:LAST - 1],
+                        in0=csum[pr][:, gi, 0:LAST - 1],
+                        scalar1=b_attn[:, ft:ft + 1],
+                        scalar2=cst[pr][:, 3 + gi, 0:1],
+                        op0=MULT,
+                        op1=ADD,
+                    )
+                    nc.gpsimd.tensor_tensor(
+                        out=far_bias[pr][:, gi, half:half + 1],
+                        in0=tap(pr, gi, CONV_TAPS[gi] - 1),
+                        in1=b_attn[:, ft:ft + 1],
+                        op=MULT,
+                    )
+
+        for pr in range(PROJ):
+            prepare_constants(pr)
+
+        x_words = x_sb[:].bitcast(F32)
+        grouped_words = grouped[:].bitcast(F32)
+        for b in range(B):
+            for tt in range(b * J, (b + 1) * J):
+                xt = x_banks.tile([P, PASSES, 2, P], F32, tag="x")
+                for g in range(PASSES):
+                    for u in range(2):
+                        nc.tensor.transpose(
+                            xt[:, g, u, :],
+                            x_words[:, tt, 256 * g + u:256 * (g + 1):2],
+                            ident[:],
+                        )
+                copy = nc.vector.tensor_copy if tt % 2 == 0 else nc.scalar.copy
+                copy(
+                    out=grouped_words[:, :, tt * P:(tt + 1) * P, :],
+                    in_=xt[:].rearrange("p g u t -> p g t u"),
+                )
+            for g in range(PASSES):
+                nc.vector.quantize_mx(
+                    out=x_codes[:, g, b * S:(b + 1) * S].bitcast(FP8X4),
+                    scales=x_planes[:, g, b * S:(b + 1) * S],
+                    in_=grouped[:, g, b * S:(b + 1) * S, :].rearrange("p t c -> p (t c)"),
+                )
+
+        def plain_heads(pr, b):
+            cols = slice(pr * E, pr * E + GROUP_FEATURES)
+            for pair in range(J // 2):
+                z_ps = x_banks.tile([P, 2, GROUP_FEATURES], F32, tag="x")
+                for i in range(2):
+                    tokens = slice((b * J + 2 * pair + i) * P, (b * J + 2 * pair + i + 1) * P)
+                    for g in range(PASSES):
+                        nc.tensor.matmul_mx(
+                            out=z_ps[:, i, :],
+                            lhsT=x_codes[:, g, tokens].bitcast(FP8X4),
+                            lhsT_scale=x_planes[:, g, tokens],
+                            rhs=w_codes[:, g, cols].bitcast(FP8X4),
+                            rhs_scale=w_planes[:, g, cols],
+                            start=(g == 0),
+                            stop=(g == PASSES - 1),
+                        )
+                z_sb = work.tile([P, 2, GROUP_FEATURES], F32, tag="z_sb")
+                nc.vector.tensor_tensor(
+                    out=z_sb[:],
+                    in0=z_ps[:],
+                    in1=b_plain[:, pr, :].unsqueeze(1).to_broadcast([P, 2, GROUP_FEATURES]),
+                    op=ADD,
+                )
+                for i in range(2):
+                    s0 = (2 * pair + i) * P
+                    nc.sync.dma_start(
+                        out=outs[pr][b, 0:GROUP_HEADS, s0:s0 + P, :].rearrange("h p d -> p h d"),
+                        in_=z_sb[:, i, :].rearrange("p (h d) -> p h d", d=D),
+                    )
+
+        rounds = [(pr, b, gi) for pr in range(PROJ) for b in range(B) for gi in CONV_ORDER]
+        n_rounds = len(rounds)
+        x_of = {}
+        acc_of = {}
+        split_of = {}
+        y_of = {}
+
+        def by_partition(ap):
+            return ap.rearrange("f (p j) -> f p j", j=J)
+
+        def project(r):
+            pr, b, gi = rounds[r]
+            x_of[r] = []
+            for half in range(HALVES):
+                c0 = pr * E + (gi + 1) * GROUP_FEATURES + half * P
+                x_ps = x_banks.tile([P, S], F32, tag="x")
+                for g in range(PASSES):
+                    nc.tensor.matmul_mx(
+                        out=x_ps[:],
+                        lhsT=w_codes[:, g, c0:c0 + P].bitcast(FP8X4),
+                        lhsT_scale=w_planes[:, g, c0:c0 + P],
+                        rhs=x_codes[:, g, b * S:(b + 1) * S].bitcast(FP8X4),
+                        rhs_scale=x_planes[:, g, b * S:(b + 1) * S],
+                        start=(g == 0),
+                        stop=(g == PASSES - 1),
+                    )
+                x_of[r].append(x_ps)
+
+        def head(r):
+            pr, b, gi = rounds[r]
+            far = CONV_TAPS[gi] - 1
+            first = far - 1
+            acc = sums.tile([P, HALVES, S], F32, tag="acc")
+            acc_of[r] = acc
+            nc.scalar.copy(out=acc[:, :, 0:first], in_=bias[pr][:, gi, :, 0:first])
+            for half in range(HALVES):
+                nc.scalar.activation(
+                    out=acc[:, half, first:S],
+                    in_=x_of[r][half][:, 0:S - first],
+                    func=IDENTITY,
+                    bias=bias[pr][:, gi, half, first:first + 1],
+                    scale=tap(pr, gi, first),
+                )
+            for half in range(HALVES):
+                nc.scalar.activation(
+                    out=far_ring[r % len(far_ring)][:, half, :, PAD:PAD + P].rearrange("f j p -> f p j"),
+                    in_=by_partition(x_of[r][half][:]),
+                    func=IDENTITY,
+                    bias=far_bias[pr][:, gi, half:half + 1],
+                    scale=tap(pr, gi, far),
+                )
+
+        def chain(r):
+            pr, b, gi = rounds[r]
+            acc = acc_of[r]
+            split = work.tile([P, HALVES, J, P], F32, tag="split")
+            split_of[r] = split
+            for back in range(CONV_TAPS[gi] - 3, 0, -1):
+                for half in range(HALVES):
+                    nc.vector.scalar_tensor_tensor(
+                        out=acc[:, half, back:S],
+                        in0=x_of[r][half][:, 0:S - back],
+                        scalar=tap(pr, gi, back),
+                        in1=acc[:, half, back:S],
+                        op0=MULT,
+                        op1=ADD,
+                    )
+            for half in range(HALVES):
+                nc.vector.scalar_tensor_tensor(
+                    out=split[:, half, :, :].rearrange("f j p -> f p j"),
+                    in0=by_partition(x_of[r][half][:]),
+                    scalar=tap(pr, gi, 0),
+                    in1=by_partition(acc[:, half, :]),
+                    op0=MULT,
+                    op1=ADD,
+                )
+
+        def turn(r):
+            pr, b, gi = rounds[r]
+            far = CONV_TAPS[gi] - 1
+            far_tile = far_ring[r % len(far_ring)]
+            y_of[r] = []
+            for half in range(HALVES):
+                y_ps = y_banks.tile([P, J, P], F32, tag="y")
+                for j in range(J):
+                    j_far = (j - far) % J
+                    carry = (far - j + j_far) // J
+                    nc.tensor.matmul(
+                        y_ps[:, j, :], lhsT=split_of[r][:, half, j, :], rhs=ident[:],
+                        is_transpose=True, start=True, stop=False,
+                    )
+                    nc.tensor.matmul(
+                        y_ps[:, j, :], lhsT=far_tile[:, half, j_far, PAD - carry:PAD - carry + P], rhs=ident[:],
+                        is_transpose=True, start=False, stop=True,
+                    )
+                y_of[r].append(y_ps)
+
+        def store(r):
+            pr, b, gi = rounds[r]
+            h0 = (gi + 1) * GROUP_HEADS
+            y_sb = work.tile([P, HALVES, P // D, J, D], F32, tag="y_sb")
+            for half in range(HALVES):
+                nc.scalar.copy(out=y_sb[:, half], in_=y_of[r][half][:].rearrange("p j (h d) -> p h j d", d=D))
+            nc.sync.dma_start(
+                out=outs[pr][b, h0:h0 + GROUP_HEADS, :, :].rearrange("h (p j) d -> p h (j d)", j=J),
+                in_=y_sb[:].rearrange("p t h j d -> p (t h) (j d)"),
+            )
+
+        for r in range(AHEAD):
+            project(r)
+            head(r)
+        for r in range(n_rounds):
+            pr, b, gi = rounds[r]
+            chain(r)
+            if gi == CONV_ORDER[0]:
+                plain_heads(pr, b)
+            if r + AHEAD < n_rounds:
+                project(r + AHEAD)
+                head(r + AHEAD)
+            turn(r)
+            store(r)

@@ -25,9 +25,9 @@ FEATURE_TILES = PROJ * E // P
 J = S // P
 SLOT = 16
 LAST = 8
-PAD = 8
 CONV_ORDER = (2, 1, 0)
 AHEAD = 3
+MOST_SHARED = 2
 
 FLOPS = 2 * B * S * E * PROJ * E
 
@@ -45,6 +45,9 @@ def tile_tranceptionblockattention_pa_kernel(
     conv_b = ((qb3, qb5, qb7), (kb3, kb5, kb7), (vb3, vb5, vb7))
     outs = (out_0, out_1, out_2)
 
+    def shared_taps(taps):
+        return (taps - 3) // 2
+
     with tc.tile_pool(name="keep", bufs=1) as keep, \
             tc.tile_pool(name="work", bufs=3) as work, \
             tc.tile_pool(name="sums", bufs=AHEAD + 2) as sums, \
@@ -61,14 +64,12 @@ def tile_tranceptionblockattention_pa_kernel(
         w_planes = keep.tile([P, PASSES, PROJ * E], U8, align_bytes=64)
         b_rows_bf = keep.tile([P, P], BF16)
         b_rows = keep.tile([P, P], F32)
-        b_attn = keep.tile([P, FEATURE_TILES], F32)
+        b_attn = keep.tile([P, PROJ, 4, HALVES], F32)
         b_plain = keep.tile([P, PROJ, GROUP_FEATURES], BF16)
         cst_bf = [keep.tile([P, 6, SLOT], BF16, name="cst_bf%d" % pr) for pr in range(PROJ)]
         cst = [keep.tile([P, 6, SLOT], F32, name="cst%d" % pr) for pr in range(PROJ)]
         csum = [keep.tile([P, 3, LAST], F32, name="csum%d" % pr) for pr in range(PROJ)]
         bias = [keep.tile([P, 3, HALVES, LAST], F32, name="bias%d" % pr) for pr in range(PROJ)]
-        far_bias = [keep.tile([P, 3, HALVES], F32, name="far_bias%d" % pr) for pr in range(PROJ)]
-        far_ring = [keep.tile([P, HALVES, J, PAD + P], F32, name="far%d" % i) for i in range(AHEAD + 2)]
 
         nc.vector.memset(cst_bf[0][:], 0.0)
         nc.vector.memset(b_rows_bf[:], 0.0)
@@ -76,8 +77,6 @@ def tile_tranceptionblockattention_pa_kernel(
         nc.vector.memset(cst_bf[1][:], 0.0)
         nc.vector.memset(cst_bf[2][:], 0.0)
         make_identity(nc, ident[:])
-        for far_tile in far_ring:
-            nc.gpsimd.memset(far_tile[:, :, :, 0:PAD], 0.0)
 
         x_rows = hidden_states.flatten_outer_dims().rearrange("(t p) k -> p t k", p=P)
 
@@ -120,41 +119,32 @@ def tile_tranceptionblockattention_pa_kernel(
         nc.vector.tensor_copy(out=b_rows[:], in_=b_rows_bf[:])
         b_cols = x_banks.tile([P, S], F32, tag="x")
         nc.tensor.transpose(b_cols[:, 0:P], b_rows[:], ident[:])
-        nc.vector.tensor_copy(out=b_attn[:], in_=b_cols[:, 0:FEATURE_TILES])
+        nc.vector.tensor_copy(out=b_attn[:].rearrange("p r g t -> p (r g t)"), in_=b_cols[:, 0:FEATURE_TILES])
 
         def tap(pr, gi, back):
             return cst[pr][:, gi, LAST - 1 - back:LAST - back]
 
         def prepare_constants(pr):
+            shape = [P, 3, HALVES, LAST]
+            b_here = b_attn[:, pr, 1:4, :].unsqueeze(3).to_broadcast(shape)
             nc.gpsimd.tensor_copy(out=cst[pr][:], in_=cst_bf[pr][:])
             nc.gpsimd.tensor_copy(out=csum[pr][:, :, 0:1], in_=cst[pr][:, 0:3, LAST - 1:LAST])
-            for s in range(1, LAST - 1):
+            for s in range(1, LAST):
                 nc.gpsimd.tensor_tensor(
                     out=csum[pr][:, :, s:s + 1],
                     in0=csum[pr][:, :, s - 1:s],
                     in1=cst[pr][:, 0:3, LAST - 1 - s:LAST - s],
                     op=ADD,
                 )
-            for gi in CONV_ORDER:
-                for half in range(HALVES):
-                    ft = (pr * E + (gi + 1) * GROUP_FEATURES) // P + half
-                    nc.gpsimd.tensor_scalar(
-                        out=bias[pr][:, gi, half, 0:LAST - 1],
-                        in0=csum[pr][:, gi, 0:LAST - 1],
-                        scalar1=b_attn[:, ft:ft + 1],
-                        scalar2=cst[pr][:, 3 + gi, 0:1],
-                        op0=MULT,
-                        op1=ADD,
-                    )
-                    nc.gpsimd.tensor_tensor(
-                        out=far_bias[pr][:, gi, half:half + 1],
-                        in0=tap(pr, gi, CONV_TAPS[gi] - 1),
-                        in1=b_attn[:, ft:ft + 1],
-                        op=MULT,
-                    )
+            nc.gpsimd.tensor_tensor(
+                out=bias[pr][:], in0=csum[pr][:].unsqueeze(2).to_broadcast(shape), in1=b_here, op=MULT,
+            )
+            nc.gpsimd.tensor_tensor(
+                out=bias[pr][:], in0=bias[pr][:],
+                in1=cst[pr][:, 3:6, 0:1].unsqueeze(2).to_broadcast(shape), op=ADD,
+            )
 
-        for pr in range(PROJ):
-            prepare_constants(pr)
+        prepare_constants(0)
 
         x_words = x_sb[:].bitcast(F32)
         grouped_words = grouped[:].bitcast(F32)
@@ -180,42 +170,51 @@ def tile_tranceptionblockattention_pa_kernel(
                     in_=grouped[:, g, b * S:(b + 1) * S, :].rearrange("p t c -> p (t c)"),
                 )
 
-        def plain_heads(pr, b):
-            cols = slice(pr * E, pr * E + GROUP_FEATURES)
-            for pair in range(J // 2):
-                z_ps = x_banks.tile([P, 2, GROUP_FEATURES], F32, tag="x")
-                for i in range(2):
-                    tokens = slice((b * J + 2 * pair + i) * P, (b * J + 2 * pair + i + 1) * P)
-                    for g in range(PASSES):
-                        nc.tensor.matmul_mx(
-                            out=z_ps[:, i, :],
-                            lhsT=x_codes[:, g, tokens].bitcast(FP8X4),
-                            lhsT_scale=x_planes[:, g, tokens],
-                            rhs=w_codes[:, g, cols].bitcast(FP8X4),
-                            rhs_scale=w_planes[:, g, cols],
-                            start=(g == 0),
-                            stop=(g == PASSES - 1),
-                        )
-                z_sb = work.tile([P, 2, GROUP_FEATURES], F32, tag="z_sb")
-                nc.vector.tensor_tensor(
-                    out=z_sb[:],
-                    in0=z_ps[:],
-                    in1=b_plain[:, pr, :].unsqueeze(1).to_broadcast([P, 2, GROUP_FEATURES]),
-                    op=ADD,
-                )
-                for i in range(2):
-                    s0 = (2 * pair + i) * P
-                    nc.sync.dma_start(
-                        out=outs[pr][b, 0:GROUP_HEADS, s0:s0 + P, :].rearrange("h p d -> p h d"),
-                        in_=z_sb[:, i, :].rearrange("p (h d) -> p h d", d=D),
-                    )
-
         rounds = [(pr, b, gi) for pr in range(PROJ) for b in range(B) for gi in CONV_ORDER]
         n_rounds = len(rounds)
         x_of = {}
         acc_of = {}
         split_of = {}
         y_of = {}
+        z_of = {}
+
+        def has_plain(r):
+            return rounds[r][2] != CONV_ORDER[0]
+
+        def plain_project(r):
+            pr, b, gi = rounds[r]
+            first_tile = b * J + 2 * (CONV_ORDER.index(gi) - 1)
+            cols = slice(pr * E, pr * E + GROUP_FEATURES)
+            z_ps = y_banks.tile([P, 2, GROUP_FEATURES], F32, tag="y")
+            z_of[r] = z_ps
+            for i in range(2):
+                tokens = slice((first_tile + i) * P, (first_tile + i + 1) * P)
+                for g in range(PASSES):
+                    nc.tensor.matmul_mx(
+                        out=z_ps[:, i, :],
+                        lhsT=x_codes[:, g, tokens].bitcast(FP8X4),
+                        lhsT_scale=x_planes[:, g, tokens],
+                        rhs=w_codes[:, g, cols].bitcast(FP8X4),
+                        rhs_scale=w_planes[:, g, cols],
+                        start=(g == 0),
+                        stop=(g == PASSES - 1),
+                    )
+
+        def plain_finish(r):
+            pr, b, gi = rounds[r]
+            z_sb = work.tile([P, 2, GROUP_FEATURES], F32, tag="z_sb")
+            nc.vector.tensor_tensor(
+                out=z_sb[:],
+                in0=z_of[r][:],
+                in1=b_plain[:, pr, :].unsqueeze(1).to_broadcast([P, 2, GROUP_FEATURES]),
+                op=ADD,
+            )
+            for i in range(2):
+                s0 = (2 * (CONV_ORDER.index(gi) - 1) + i) * P
+                nc.sync.dma_start(
+                    out=outs[pr][b, 0:GROUP_HEADS, s0:s0 + P, :].rearrange("h p d -> p h d"),
+                    in_=z_sb[:, i, :].rearrange("p (h d) -> p h d", d=D),
+                )
 
         def by_partition(ap):
             return ap.rearrange("f (p j) -> f p j", j=J)
@@ -241,33 +240,39 @@ def tile_tranceptionblockattention_pa_kernel(
         def head(r):
             pr, b, gi = rounds[r]
             far = CONV_TAPS[gi] - 1
-            first = far - 1
             acc = sums.tile([P, HALVES, S], F32, tag="acc")
             acc_of[r] = acc
-            nc.scalar.copy(out=acc[:, :, 0:first], in_=bias[pr][:, gi, :, 0:first])
+            if shared_taps(CONV_TAPS[gi]) > 0:
+                extra = work.tile([P, HALVES, MOST_SHARED, S], F32, tag="extra")
+            nc.scalar.copy(out=acc[:, :, 0:far], in_=bias[pr][:, gi, :, 0:far])
             for half in range(HALVES):
                 nc.scalar.activation(
-                    out=acc[:, half, first:S],
-                    in_=x_of[r][half][:, 0:S - first],
+                    out=acc[:, half, far:S],
+                    in_=x_of[r][half][:, 0:S - far],
                     func=IDENTITY,
-                    bias=bias[pr][:, gi, half, first:first + 1],
-                    scale=tap(pr, gi, first),
-                )
-            for half in range(HALVES):
-                nc.scalar.activation(
-                    out=far_ring[r % len(far_ring)][:, half, :, PAD:PAD + P].rearrange("f j p -> f p j"),
-                    in_=by_partition(x_of[r][half][:]),
-                    func=IDENTITY,
-                    bias=far_bias[pr][:, gi, half:half + 1],
+                    bias=bias[pr][:, gi, half, far:far + 1],
                     scale=tap(pr, gi, far),
                 )
+                for k in range(shared_taps(CONV_TAPS[gi])):
+                    back = far - 1 - k
+                    nc.scalar.activation(
+                        out=extra[:, half, k, back:S],
+                        in_=x_of[r][half][:, 0:S - back],
+                        func=IDENTITY,
+                        bias=0.0,
+                        scale=tap(pr, gi, back),
+                    )
+                    nc.gpsimd.tensor_tensor(
+                        out=acc[:, half, back:S], in0=acc[:, half, back:S], in1=extra[:, half, k, back:S], op=ADD,
+                    )
 
         def chain(r):
             pr, b, gi = rounds[r]
+            taps = CONV_TAPS[gi]
             acc = acc_of[r]
             split = work.tile([P, HALVES, J, P], F32, tag="split")
             split_of[r] = split
-            for back in range(CONV_TAPS[gi] - 3, 0, -1):
+            for back in range(taps - 2 - shared_taps(taps), 0, -1):
                 for half in range(HALVES):
                     nc.vector.scalar_tensor_tensor(
                         out=acc[:, half, back:S],
@@ -288,35 +293,23 @@ def tile_tranceptionblockattention_pa_kernel(
                 )
 
         def turn(r):
-            pr, b, gi = rounds[r]
-            far = CONV_TAPS[gi] - 1
-            far_tile = far_ring[r % len(far_ring)]
             y_of[r] = []
             for half in range(HALVES):
                 y_ps = y_banks.tile([P, J, P], F32, tag="y")
                 for j in range(J):
-                    j_far = (j - far) % J
-                    carry = (far - j + j_far) // J
-                    nc.tensor.matmul(
-                        y_ps[:, j, :], lhsT=split_of[r][:, half, j, :], rhs=ident[:],
-                        is_transpose=True, start=True, stop=False,
-                    )
-                    nc.tensor.matmul(
-                        y_ps[:, j, :], lhsT=far_tile[:, half, j_far, PAD - carry:PAD - carry + P], rhs=ident[:],
-                        is_transpose=True, start=False, stop=True,
-                    )
+                    nc.tensor.transpose(y_ps[:, j, :], split_of[r][:, half, j, :], ident[:])
                 y_of[r].append(y_ps)
 
         def store(r):
             pr, b, gi = rounds[r]
-            h0 = (gi + 1) * GROUP_HEADS
-            y_sb = work.tile([P, HALVES, P // D, J, D], F32, tag="y_sb")
             for half in range(HALVES):
-                nc.scalar.copy(out=y_sb[:, half], in_=y_of[r][half][:].rearrange("p j (h d) -> p h j d", d=D))
-            nc.sync.dma_start(
-                out=outs[pr][b, h0:h0 + GROUP_HEADS, :, :].rearrange("h (p j) d -> p h (j d)", j=J),
-                in_=y_sb[:].rearrange("p t h j d -> p (t h) (j d)"),
-            )
+                h0 = (gi + 1) * GROUP_HEADS + half * (P // D)
+                y_sb = work.tile([P, P // D, J, D], F32, tag="y_sb")
+                nc.scalar.copy(out=y_sb[:], in_=y_of[r][half][:].rearrange("p j (h d) -> p h j d", d=D))
+                nc.sync.dma_start(
+                    out=outs[pr][b, h0:h0 + P // D, :, :].rearrange("h (p j) d -> p h (j d)", j=J),
+                    in_=y_sb[:].rearrange("p h j d -> p h (j d)"),
+                )
 
         for r in range(AHEAD):
             project(r)
@@ -324,10 +317,14 @@ def tile_tranceptionblockattention_pa_kernel(
         for r in range(n_rounds):
             pr, b, gi = rounds[r]
             chain(r)
-            if gi == CONV_ORDER[0]:
-                plain_heads(pr, b)
+            if has_plain(r):
+                plain_finish(r)
             if r + AHEAD < n_rounds:
                 project(r + AHEAD)
                 head(r + AHEAD)
             turn(r)
             store(r)
+            if r + 1 < n_rounds and has_plain(r + 1):
+                plain_project(r + 1)
+            if b == 0 and gi == CONV_ORDER[-1] and pr + 1 < PROJ:
+                prepare_constants(pr + 1)

@@ -25,6 +25,7 @@ FEATURE_TILES = PROJ * E // P
 J = S // P
 SLOT = 16
 LAST = 8
+PAD = 8
 CONV_ORDER = (2, 1, 0)
 AHEAD = 3
 MOST_SHARED = 2
@@ -70,6 +71,8 @@ def tile_tranceptionblockattention_pa_kernel(
         cst = [keep.tile([P, 6, SLOT], F32, name="cst%d" % pr) for pr in range(PROJ)]
         csum = [keep.tile([P, 3, LAST], F32, name="csum%d" % pr) for pr in range(PROJ)]
         bias = [keep.tile([P, 3, HALVES, LAST], F32, name="bias%d" % pr) for pr in range(PROJ)]
+        tap_bias = [keep.tile([P, 3, HALVES, LAST], F32, name="tap_bias%d" % pr) for pr in range(PROJ)]
+        far_ring = [keep.tile([P, HALVES, MOST_SHARED, J, PAD + P], F32, name="far%d" % i) for i in range(AHEAD + 2)]
 
         nc.vector.memset(cst_bf[0][:], 0.0)
         nc.vector.memset(b_rows_bf[:], 0.0)
@@ -77,6 +80,8 @@ def tile_tranceptionblockattention_pa_kernel(
         nc.vector.memset(cst_bf[1][:], 0.0)
         nc.vector.memset(cst_bf[2][:], 0.0)
         make_identity(nc, ident[:])
+        for far_tile in far_ring:
+            nc.gpsimd.memset(far_tile[:, :, :, :, 0:PAD], 0.0)
 
         x_rows = hidden_states.flatten_outer_dims().rearrange("(t p) k -> p t k", p=P)
 
@@ -143,8 +148,13 @@ def tile_tranceptionblockattention_pa_kernel(
                 out=bias[pr][:], in0=bias[pr][:],
                 in1=cst[pr][:, 3:6, 0:1].unsqueeze(2).to_broadcast(shape), op=ADD,
             )
+            nc.gpsimd.tensor_tensor(
+                out=tap_bias[pr][:], in0=cst[pr][:, 0:3, 0:LAST].unsqueeze(2).to_broadcast(shape), in1=b_here, op=MULT,
+            )
 
         prepare_constants(0)
+        prepare_constants(1)
+        prepare_constants(2)
 
         x_words = x_sb[:].bitcast(F32)
         grouped_words = grouped[:].bitcast(F32)
@@ -178,43 +188,40 @@ def tile_tranceptionblockattention_pa_kernel(
         y_of = {}
         z_of = {}
 
-        def has_plain(r):
-            return rounds[r][2] != CONV_ORDER[0]
-
-        def plain_project(r):
-            pr, b, gi = rounds[r]
-            first_tile = b * J + 2 * (CONV_ORDER.index(gi) - 1)
+        def plain_project(pr, b):
             cols = slice(pr * E, pr * E + GROUP_FEATURES)
-            z_ps = y_banks.tile([P, 2, GROUP_FEATURES], F32, tag="y")
-            z_of[r] = z_ps
-            for i in range(2):
-                tokens = slice((first_tile + i) * P, (first_tile + i + 1) * P)
-                for g in range(PASSES):
-                    nc.tensor.matmul_mx(
-                        out=z_ps[:, i, :],
-                        lhsT=x_codes[:, g, tokens].bitcast(FP8X4),
-                        lhsT_scale=x_planes[:, g, tokens],
-                        rhs=w_codes[:, g, cols].bitcast(FP8X4),
-                        rhs_scale=w_planes[:, g, cols],
-                        start=(g == 0),
-                        stop=(g == PASSES - 1),
-                    )
+            z_of[(pr, b)] = []
+            for pair in range(J // 2):
+                z_ps = x_banks.tile([P, 2, GROUP_FEATURES], F32, tag="x")
+                for i in range(2):
+                    tokens = slice((b * J + 2 * pair + i) * P, (b * J + 2 * pair + i + 1) * P)
+                    for g in range(PASSES):
+                        nc.tensor.matmul_mx(
+                            out=z_ps[:, i, :],
+                            lhsT=x_codes[:, g, tokens].bitcast(FP8X4),
+                            lhsT_scale=x_planes[:, g, tokens],
+                            rhs=w_codes[:, g, cols].bitcast(FP8X4),
+                            rhs_scale=w_planes[:, g, cols],
+                            start=(g == 0),
+                            stop=(g == PASSES - 1),
+                        )
+                z_of[(pr, b)].append(z_ps)
 
-        def plain_finish(r):
-            pr, b, gi = rounds[r]
-            z_sb = work.tile([P, 2, GROUP_FEATURES], F32, tag="z_sb")
-            nc.vector.tensor_tensor(
-                out=z_sb[:],
-                in0=z_of[r][:],
-                in1=b_plain[:, pr, :].unsqueeze(1).to_broadcast([P, 2, GROUP_FEATURES]),
-                op=ADD,
-            )
-            for i in range(2):
-                s0 = (2 * (CONV_ORDER.index(gi) - 1) + i) * P
-                nc.sync.dma_start(
-                    out=outs[pr][b, 0:GROUP_HEADS, s0:s0 + P, :].rearrange("h p d -> p h d"),
-                    in_=z_sb[:, i, :].rearrange("p (h d) -> p h d", d=D),
+        def plain_finish(pr, b):
+            for pair in range(J // 2):
+                z_sb = work.tile([P, 2, GROUP_FEATURES], F32, tag="z_sb")
+                nc.vector.tensor_tensor(
+                    out=z_sb[:],
+                    in0=z_of[(pr, b)][pair][:],
+                    in1=b_plain[:, pr, :].unsqueeze(1).to_broadcast([P, 2, GROUP_FEATURES]),
+                    op=ADD,
                 )
+                for i in range(2):
+                    s0 = (2 * pair + i) * P
+                    nc.sync.dma_start(
+                        out=outs[pr][b, 0:GROUP_HEADS, s0:s0 + P, :].rearrange("h p d -> p h d"),
+                        in_=z_sb[:, i, :].rearrange("p (h d) -> p h d", d=D),
+                    )
 
         def by_partition(ap):
             return ap.rearrange("f (p j) -> f p j", j=J)
@@ -239,92 +246,109 @@ def tile_tranceptionblockattention_pa_kernel(
 
         def head(r):
             pr, b, gi = rounds[r]
-            far = CONV_TAPS[gi] - 1
+            taps = CONV_TAPS[gi]
+            first = taps - 1 - shared_taps(taps)
             acc = sums.tile([P, HALVES, S], F32, tag="acc")
             acc_of[r] = acc
-            if shared_taps(CONV_TAPS[gi]) > 0:
-                extra = work.tile([P, HALVES, MOST_SHARED, S], F32, tag="extra")
-            nc.scalar.copy(out=acc[:, :, 0:far], in_=bias[pr][:, gi, :, 0:far])
+            nc.scalar.copy(out=acc[:, :, 0:first], in_=bias[pr][:, gi, :, 0:first])
             for half in range(HALVES):
                 nc.scalar.activation(
-                    out=acc[:, half, far:S],
-                    in_=x_of[r][half][:, 0:S - far],
+                    out=acc[:, half, first:S],
+                    in_=x_of[r][half][:, 0:S - first],
                     func=IDENTITY,
-                    bias=bias[pr][:, gi, half, far:far + 1],
-                    scale=tap(pr, gi, far),
+                    bias=bias[pr][:, gi, half, first:first + 1],
+                    scale=tap(pr, gi, first),
                 )
-                for k in range(shared_taps(CONV_TAPS[gi])):
-                    back = far - 1 - k
+            for k in range(shared_taps(taps)):
+                back = first + 1 + k
+                for half in range(HALVES):
                     nc.scalar.activation(
-                        out=extra[:, half, k, back:S],
-                        in_=x_of[r][half][:, 0:S - back],
+                        out=far_ring[r % len(far_ring)][:, half, k, :, PAD:PAD + P].rearrange("f j p -> f p j"),
+                        in_=by_partition(x_of[r][half][:]),
                         func=IDENTITY,
-                        bias=0.0,
+                        bias=tap_bias[pr][:, gi, half, LAST - 1 - back:LAST - back],
                         scale=tap(pr, gi, back),
                     )
-                    nc.gpsimd.tensor_tensor(
-                        out=acc[:, half, back:S], in0=acc[:, half, back:S], in1=extra[:, half, k, back:S], op=ADD,
-                    )
 
-        def chain(r):
+        def vector_taps(r):
+            taps = CONV_TAPS[rounds[r][2]]
+            return list(range(taps - 2 - shared_taps(taps), -1, -1))
+
+        def chain(r, backs):
             pr, b, gi = rounds[r]
-            taps = CONV_TAPS[gi]
             acc = acc_of[r]
-            split = work.tile([P, HALVES, J, P], F32, tag="split")
-            split_of[r] = split
-            for back in range(taps - 2 - shared_taps(taps), 0, -1):
-                for half in range(HALVES):
-                    nc.vector.scalar_tensor_tensor(
-                        out=acc[:, half, back:S],
-                        in0=x_of[r][half][:, 0:S - back],
-                        scalar=tap(pr, gi, back),
-                        in1=acc[:, half, back:S],
-                        op0=MULT,
-                        op1=ADD,
-                    )
-            for half in range(HALVES):
-                nc.vector.scalar_tensor_tensor(
-                    out=split[:, half, :, :].rearrange("f j p -> f p j"),
-                    in0=by_partition(x_of[r][half][:]),
-                    scalar=tap(pr, gi, 0),
-                    in1=by_partition(acc[:, half, :]),
-                    op0=MULT,
-                    op1=ADD,
-                )
+            for back in backs:
+                if back > 0:
+                    for half in range(HALVES):
+                        nc.vector.scalar_tensor_tensor(
+                            out=acc[:, half, back:S],
+                            in0=x_of[r][half][:, 0:S - back],
+                            scalar=tap(pr, gi, back),
+                            in1=acc[:, half, back:S],
+                            op0=MULT,
+                            op1=ADD,
+                        )
+                else:
+                    split = work.tile([P, HALVES, J, P], F32, tag="split")
+                    split_of[r] = split
+                    for half in range(HALVES):
+                        nc.vector.scalar_tensor_tensor(
+                            out=split[:, half, :, :].rearrange("f j p -> f p j"),
+                            in0=by_partition(x_of[r][half][:]),
+                            scalar=tap(pr, gi, 0),
+                            in1=by_partition(acc[:, half, :]),
+                            op0=MULT,
+                            op1=ADD,
+                        )
 
         def turn(r):
+            pr, b, gi = rounds[r]
+            taps = CONV_TAPS[gi]
+            n_far = shared_taps(taps)
+            far_tile = far_ring[r % len(far_ring)]
             y_of[r] = []
             for half in range(HALVES):
                 y_ps = y_banks.tile([P, J, P], F32, tag="y")
                 for j in range(J):
-                    nc.tensor.transpose(y_ps[:, j, :], split_of[r][:, half, j, :], ident[:])
+                    nc.tensor.matmul(
+                        y_ps[:, j, :], lhsT=split_of[r][:, half, j, :], rhs=ident[:],
+                        is_transpose=True, start=True, stop=(n_far == 0),
+                    )
+                    for k in range(n_far):
+                        back = taps - n_far + k
+                        j_far = (j - back) % J
+                        carry = (back - j + j_far) // J
+                        nc.tensor.matmul(
+                            y_ps[:, j, :], lhsT=far_tile[:, half, k, j_far, PAD - carry:PAD - carry + P], rhs=ident[:],
+                            is_transpose=True, start=False, stop=(k == n_far - 1),
+                        )
                 y_of[r].append(y_ps)
 
         def store(r):
             pr, b, gi = rounds[r]
+            h0 = (gi + 1) * GROUP_HEADS
+            y_sb = work.tile([P, HALVES, P // D, J, D], F32, tag="y_sb")
             for half in range(HALVES):
-                h0 = (gi + 1) * GROUP_HEADS + half * (P // D)
-                y_sb = work.tile([P, P // D, J, D], F32, tag="y_sb")
-                nc.scalar.copy(out=y_sb[:], in_=y_of[r][half][:].rearrange("p j (h d) -> p h j d", d=D))
-                nc.sync.dma_start(
-                    out=outs[pr][b, h0:h0 + P // D, :, :].rearrange("h (p j) d -> p h (j d)", j=J),
-                    in_=y_sb[:].rearrange("p h j d -> p h (j d)"),
-                )
+                nc.scalar.copy(out=y_sb[:, half], in_=y_of[r][half][:].rearrange("p j (h d) -> p h j d", d=D))
+            nc.sync.dma_start(
+                out=outs[pr][b, h0:h0 + GROUP_HEADS, :, :].rearrange("h (p j) d -> p h (j d)", j=J),
+                in_=y_sb[:].rearrange("p t h j d -> p (t h) (j d)"),
+            )
 
         for r in range(AHEAD):
             project(r)
             head(r)
         for r in range(n_rounds):
             pr, b, gi = rounds[r]
-            chain(r)
-            if has_plain(r):
-                plain_finish(r)
+            backs = vector_taps(r)
+            chain(r, backs[:1])
+            if gi == CONV_ORDER[1]:
+                plain_finish(pr, b)
+            chain(r, backs[1:])
+            if gi == CONV_ORDER[0]:
+                plain_project(pr, b)
             if r + AHEAD < n_rounds:
                 project(r + AHEAD)
                 head(r + AHEAD)
             turn(r)
             store(r)
-            if r + 1 < n_rounds and has_plain(r + 1):
-                plain_project(r + 1)
-            if b == 0 and gi == CONV_ORDER[-1] and pr + 1 < PROJ:
-                prepare_constants(pr + 1)

@@ -24,7 +24,7 @@ GROUP_HEADS = GROUP_FEATURES // D
 FEATURE_TILES = PROJ * E // P
 J = S // P
 SLOT = 16
-LAST = 8
+LAST = 9
 PAD = 8
 CONV_ORDER = (2, 1, 0)
 AHEAD = 3

@@ -28,6 +28,7 @@ LAST = 9
 PAD = 8
 CONV_ORDER = (2, 1, 0)
 AHEAD = 3
+LOOK = AHEAD * HALVES
 MOST_SHARED = 2
 
 FLOPS = 2 * B * S * E * PROJ * E
@@ -50,7 +51,7 @@ def tile_tranceptionblockattention_pa_kernel(
         return (taps - 3) // 2
 
     with tc.tile_pool(name="keep", bufs=1) as keep, \
-            tc.tile_pool(name="work", bufs=3) as work, \
+            tc.tile_pool(name="work", bufs=4) as work, \
             tc.tile_pool(name="sums", bufs=AHEAD + 2) as sums, \
             tc.psum_pool(name="x_banks", bufs=AHEAD * HALVES) as x_banks, \
             tc.psum_pool(name="y_banks", bufs=HALVES) as y_banks, \
@@ -181,17 +182,32 @@ def tile_tranceptionblockattention_pa_kernel(
                 )
 
         rounds = [(pr, b, gi) for pr in range(PROJ) for b in range(B) for gi in CONV_ORDER]
-        n_rounds = len(rounds)
-        x_of = {}
+        tiles = []
+        for pr in range(PROJ):
+            for b in range(B):
+                for gi in CONV_ORDER:
+                    for half in range(HALVES):
+                        tiles.append(("conv", pr, b, gi, half))
+                for pair in range(J // 2):
+                    tiles.append(("plain", pr, b, pair, 0))
+        n_tiles = len(tiles)
+        bank_of = {}
         acc_of = {}
         split_of = {}
         y_of = {}
-        z_of = {}
 
-        def plain_project(pr, b):
-            cols = slice(pr * E, pr * E + GROUP_FEATURES)
-            z_of[(pr, b)] = []
-            for pair in range(J // 2):
+        def round_of(t):
+            kind, pr, b, gi, half = tiles[t]
+            return rounds.index((pr, b, gi))
+
+        def by_partition(ap):
+            return ap.rearrange("f (p j) -> f p j", j=J)
+
+        def project(t):
+            kind, pr, b, gi, half = tiles[t]
+            if kind == "plain":
+                pair = gi
+                cols = slice(pr * E, pr * E + GROUP_FEATURES)
                 z_ps = x_banks.tile([P, 2, GROUP_FEATURES], F32, tag="x")
                 for i in range(2):
                     tokens = slice((b * J + 2 * pair + i) * P, (b * J + 2 * pair + i + 1) * P)
@@ -205,14 +221,65 @@ def tile_tranceptionblockattention_pa_kernel(
                             start=(g == 0),
                             stop=(g == PASSES - 1),
                         )
-                z_of[(pr, b)].append(z_ps)
+                bank_of[t] = z_ps
+                return
+            c0 = pr * E + (gi + 1) * GROUP_FEATURES + half * P
+            x_ps = x_banks.tile([P, S], F32, tag="x")
+            for g in range(PASSES):
+                nc.tensor.matmul_mx(
+                    out=x_ps[:],
+                    lhsT=w_codes[:, g, c0:c0 + P].bitcast(FP8X4),
+                    lhsT_scale=w_planes[:, g, c0:c0 + P],
+                    rhs=x_codes[:, g, b * S:(b + 1) * S].bitcast(FP8X4),
+                    rhs_scale=x_planes[:, g, b * S:(b + 1) * S],
+                    start=(g == 0),
+                    stop=(g == PASSES - 1),
+                )
+            bank_of[t] = x_ps
 
-        def plain_finish(pr, b):
-            for pair in range(J // 2):
+        def head(t):
+            kind, pr, b, gi, half = tiles[t]
+            if kind == "plain":
+                return
+            r = round_of(t)
+            taps = CONV_TAPS[gi]
+            first = taps - 1 - shared_taps(taps)
+            if half == 0:
+                acc = sums.tile([P, HALVES, S], F32, tag="acc")
+                acc_of[r] = acc
+                nc.scalar.copy(out=acc[:, :, 0:first], in_=bias[pr][:, gi, :, 0:first])
+            nc.scalar.activation(
+                out=acc_of[r][:, half, first:S],
+                in_=bank_of[t][:, 0:S - first],
+                func=IDENTITY,
+                bias=bias[pr][:, gi, half, first:first + 1],
+                scale=tap(pr, gi, first),
+            )
+            for k in range(shared_taps(taps)):
+                back = first + 1 + k
+                nc.scalar.activation(
+                    out=far_ring[r % len(far_ring)][:, half, k, :, PAD:PAD + P].rearrange("f j p -> f p j"),
+                    in_=by_partition(bank_of[t][:]),
+                    func=IDENTITY,
+                    bias=tap_bias[pr][:, gi, half, LAST - 1 - back:LAST - back],
+                    scale=tap(pr, gi, back),
+                )
+
+        def vector_steps(t):
+            kind, pr, b, gi, half = tiles[t]
+            if kind == "plain":
+                return [0]
+            taps = CONV_TAPS[gi]
+            return list(range(taps - 2 - shared_taps(taps), -1, -1))
+
+        def vector_step(t, back):
+            kind, pr, b, gi, half = tiles[t]
+            if kind == "plain":
+                pair = gi
                 z_sb = work.tile([P, 2, GROUP_FEATURES], F32, tag="z_sb")
                 nc.vector.tensor_tensor(
                     out=z_sb[:],
-                    in0=z_of[(pr, b)][pair][:],
+                    in0=bank_of[t][:],
                     in1=b_plain[:, pr, :].unsqueeze(1).to_broadcast([P, 2, GROUP_FEATURES]),
                     op=ADD,
                 )
@@ -222,133 +289,103 @@ def tile_tranceptionblockattention_pa_kernel(
                         out=outs[pr][b, 0:GROUP_HEADS, s0:s0 + P, :].rearrange("h p d -> p h d"),
                         in_=z_sb[:, i, :].rearrange("p (h d) -> p h d", d=D),
                     )
-
-        def by_partition(ap):
-            return ap.rearrange("f (p j) -> f p j", j=J)
-
-        def project(r):
-            pr, b, gi = rounds[r]
-            x_of[r] = []
-            for half in range(HALVES):
-                c0 = pr * E + (gi + 1) * GROUP_FEATURES + half * P
-                x_ps = x_banks.tile([P, S], F32, tag="x")
-                for g in range(PASSES):
-                    nc.tensor.matmul_mx(
-                        out=x_ps[:],
-                        lhsT=w_codes[:, g, c0:c0 + P].bitcast(FP8X4),
-                        lhsT_scale=w_planes[:, g, c0:c0 + P],
-                        rhs=x_codes[:, g, b * S:(b + 1) * S].bitcast(FP8X4),
-                        rhs_scale=x_planes[:, g, b * S:(b + 1) * S],
-                        start=(g == 0),
-                        stop=(g == PASSES - 1),
-                    )
-                x_of[r].append(x_ps)
-
-        def head(r):
-            pr, b, gi = rounds[r]
-            taps = CONV_TAPS[gi]
-            first = taps - 1 - shared_taps(taps)
-            acc = sums.tile([P, HALVES, S], F32, tag="acc")
-            acc_of[r] = acc
-            nc.scalar.copy(out=acc[:, :, 0:first], in_=bias[pr][:, gi, :, 0:first])
-            for half in range(HALVES):
-                nc.scalar.activation(
-                    out=acc[:, half, first:S],
-                    in_=x_of[r][half][:, 0:S - first],
-                    func=IDENTITY,
-                    bias=bias[pr][:, gi, half, first:first + 1],
-                    scale=tap(pr, gi, first),
+                return
+            acc = acc_of[round_of(t)]
+            if back > 0:
+                nc.vector.scalar_tensor_tensor(
+                    out=acc[:, half, back:S],
+                    in0=bank_of[t][:, 0:S - back],
+                    scalar=tap(pr, gi, back),
+                    in1=acc[:, half, back:S],
+                    op0=MULT,
+                    op1=ADD,
                 )
-            for k in range(shared_taps(taps)):
-                back = first + 1 + k
-                for half in range(HALVES):
-                    nc.scalar.activation(
-                        out=far_ring[r % len(far_ring)][:, half, k, :, PAD:PAD + P].rearrange("f j p -> f p j"),
-                        in_=by_partition(x_of[r][half][:]),
-                        func=IDENTITY,
-                        bias=tap_bias[pr][:, gi, half, LAST - 1 - back:LAST - back],
-                        scale=tap(pr, gi, back),
-                    )
+            else:
+                split = work.tile([P, J, P], F32, tag="split")
+                split_of[t] = split
+                nc.vector.scalar_tensor_tensor(
+                    out=split[:].rearrange("f j p -> f p j"),
+                    in0=by_partition(bank_of[t][:]),
+                    scalar=tap(pr, gi, 0),
+                    in1=by_partition(acc[:, half, :]),
+                    op0=MULT,
+                    op1=ADD,
+                )
 
-        def vector_taps(r):
-            taps = CONV_TAPS[rounds[r][2]]
-            return list(range(taps - 2 - shared_taps(taps), -1, -1))
-
-        def chain(r, backs):
-            pr, b, gi = rounds[r]
-            acc = acc_of[r]
-            for back in backs:
-                if back > 0:
-                    for half in range(HALVES):
-                        nc.vector.scalar_tensor_tensor(
-                            out=acc[:, half, back:S],
-                            in0=x_of[r][half][:, 0:S - back],
-                            scalar=tap(pr, gi, back),
-                            in1=acc[:, half, back:S],
-                            op0=MULT,
-                            op1=ADD,
-                        )
-                else:
-                    split = work.tile([P, HALVES, J, P], F32, tag="split")
-                    split_of[r] = split
-                    for half in range(HALVES):
-                        nc.vector.scalar_tensor_tensor(
-                            out=split[:, half, :, :].rearrange("f j p -> f p j"),
-                            in0=by_partition(x_of[r][half][:]),
-                            scalar=tap(pr, gi, 0),
-                            in1=by_partition(acc[:, half, :]),
-                            op0=MULT,
-                            op1=ADD,
-                        )
-
-        def turn(r):
-            pr, b, gi = rounds[r]
+        def turn(t):
+            kind, pr, b, gi, half = tiles[t]
             taps = CONV_TAPS[gi]
             n_far = shared_taps(taps)
-            far_tile = far_ring[r % len(far_ring)]
-            y_of[r] = []
-            for half in range(HALVES):
-                y_ps = y_banks.tile([P, J, P], F32, tag="y")
-                for j in range(J):
+            far_tile = far_ring[round_of(t) % len(far_ring)]
+            y_ps = y_banks.tile([P, J, P], F32, tag="y")
+            for j in range(J):
+                nc.tensor.matmul(
+                    y_ps[:, j, :], lhsT=split_of[t][:, j, :], rhs=ident[:],
+                    is_transpose=True, start=True, stop=(n_far == 0),
+                )
+                for k in range(n_far):
+                    back = taps - n_far + k
+                    j_far = (j - back) % J
+                    carry = (back - j + j_far) // J
                     nc.tensor.matmul(
-                        y_ps[:, j, :], lhsT=split_of[r][:, half, j, :], rhs=ident[:],
-                        is_transpose=True, start=True, stop=(n_far == 0),
+                        y_ps[:, j, :], lhsT=far_tile[:, half, k, j_far, PAD - carry:PAD - carry + P], rhs=ident[:],
+                        is_transpose=True, start=False, stop=(k == n_far - 1),
                     )
-                    for k in range(n_far):
-                        back = taps - n_far + k
-                        j_far = (j - back) % J
-                        carry = (back - j + j_far) // J
-                        nc.tensor.matmul(
-                            y_ps[:, j, :], lhsT=far_tile[:, half, k, j_far, PAD - carry:PAD - carry + P], rhs=ident[:],
-                            is_transpose=True, start=False, stop=(k == n_far - 1),
-                        )
-                y_of[r].append(y_ps)
+            y_of[t] = y_ps
 
-        def store(r):
-            pr, b, gi = rounds[r]
-            h0 = (gi + 1) * GROUP_HEADS
-            y_sb = work.tile([P, HALVES, P // D, J, D], F32, tag="y_sb")
-            for half in range(HALVES):
-                nc.scalar.copy(out=y_sb[:, half], in_=y_of[r][half][:].rearrange("p j (h d) -> p h j d", d=D))
+        def store(t):
+            kind, pr, b, gi, half = tiles[t]
+            h0 = (gi + 1) * GROUP_HEADS + half * (P // D)
+            y_sb = work.tile([P, P // D, J, D], F32, tag="y_sb")
+            nc.scalar.copy(out=y_sb[:], in_=y_of[t][:].rearrange("p j (h d) -> p h j d", d=D))
             nc.sync.dma_start(
-                out=outs[pr][b, h0:h0 + GROUP_HEADS, :, :].rearrange("h (p j) d -> p h (j d)", j=J),
-                in_=y_sb[:].rearrange("p t h j d -> p (t h) (j d)"),
+                out=outs[pr][b, h0:h0 + P // D, :, :].rearrange("h (p j) d -> p h (j d)", j=J),
+                in_=y_sb[:].rearrange("p h j d -> p h (j d)"),
             )
 
-        for r in range(AHEAD):
-            project(r)
-            head(r)
-        for r in range(n_rounds):
-            pr, b, gi = rounds[r]
-            backs = vector_taps(r)
-            chain(r, backs[:1])
-            if gi == CONV_ORDER[1]:
-                plain_finish(pr, b)
-            chain(r, backs[1:])
-            if gi == CONV_ORDER[0]:
-                plain_project(pr, b)
-            if r + AHEAD < n_rounds:
-                project(r + AHEAD)
-                head(r + AHEAD)
-            turn(r)
-            store(r)
+        for t in range(LOOK):
+            project(t)
+            head(t)
+        state = {"projected": LOOK, "to_store": -1}
+        waiting = [0, 1]
+        lanes = [[], []]
+
+        def take(lane):
+            t = waiting[lane]
+            if t < n_tiles:
+                waiting[lane] = t + 2
+                lanes[lane] = [t] + list(reversed(vector_steps(t)))
+
+        def advance(lane):
+            t = lanes[lane][0]
+            vector_step(t, lanes[lane][-1])
+            lanes[lane] = lanes[lane][:-1]
+            if len(lanes[lane]) > 1:
+                return
+            lanes[lane] = []
+            new = state["projected"]
+            if new < n_tiles:
+                project(new)
+            if tiles[t][0] == "conv":
+                turn(t)
+            if state["to_store"] >= 0:
+                store(state["to_store"])
+                state["to_store"] = -1
+            if tiles[t][0] == "conv":
+                state["to_store"] = t
+            if new < n_tiles:
+                head(new)
+                state["projected"] = new + 1
+            take(lane)
+
+        take(0)
+        for i in range((len(lanes[0]) - 1) // 2):
+            advance(0)
+        take(1)
+        lane = 1
+        while lanes[0] or lanes[1]:
+            if lanes[lane]:
+                advance(lane)
+            lane = 1 - lane
+        if state["to_store"] >= 0:
+            store(state["to_store"])

@@ -26,10 +26,12 @@ J = S // P
 SLOT = 16
 LAST = 9
 PAD = 8
-CONV_ORDER = (2, 1, 0)
+CONV_ORDER = (2, 1)
+SLOW = 0
+SLOW_ROUNDS = 3
 AHEAD = 3
 LOOK = AHEAD * HALVES
-MOST_SHARED = 2
+MOST_SHARED = 1
 
 FLOPS = 2 * B * S * E * PROJ * E
 
@@ -48,11 +50,12 @@ def tile_tranceptionblockattention_pa_kernel(
     outs = (out_0, out_1, out_2)
 
     def shared_taps(taps):
-        return (taps - 3) // 2
+        return 1
 
     with tc.tile_pool(name="keep", bufs=1) as keep, \
-            tc.tile_pool(name="work", bufs=4) as work, \
+            tc.tile_pool(name="work", bufs=6) as work, \
             tc.tile_pool(name="sums", bufs=AHEAD + 2) as sums, \
+            tc.tile_pool(name="slow", bufs=SLOW_ROUNDS) as slow, \
             tc.psum_pool(name="x_banks", bufs=AHEAD * HALVES) as x_banks, \
             tc.psum_pool(name="y_banks", bufs=HALVES) as y_banks, \
             tc.manual_schedule():
@@ -74,6 +77,7 @@ def tile_tranceptionblockattention_pa_kernel(
         bias = [keep.tile([P, 3, HALVES, LAST], F32, name="bias%d" % pr) for pr in range(PROJ)]
         tap_bias = [keep.tile([P, 3, HALVES, LAST], F32, name="tap_bias%d" % pr) for pr in range(PROJ)]
         far_ring = [keep.tile([P, HALVES, MOST_SHARED, J, PAD + P], F32, name="far%d" % i) for i in range(AHEAD + 2)]
+        xs_ring = [keep.tile([P, HALVES, PAD + S], F32, name="xs%d" % i) for i in range(SLOW_ROUNDS)]
 
         nc.vector.memset(cst_bf[0][:], 0.0)
         nc.vector.memset(b_rows_bf[:], 0.0)
@@ -83,6 +87,8 @@ def tile_tranceptionblockattention_pa_kernel(
         make_identity(nc, ident[:])
         for far_tile in far_ring:
             nc.gpsimd.memset(far_tile[:, :, :, :, 0:PAD], 0.0)
+        for xs_tile in xs_ring:
+            nc.gpsimd.memset(xs_tile[:, :, 0:PAD], 0.0)
 
         x_rows = hidden_states.flatten_outer_dims().rearrange("(t p) k -> p t k", p=P)
 
@@ -98,29 +104,30 @@ def tile_tranceptionblockattention_pa_kernel(
                     in_=conv_b[pr][gi].rearrange("(d o) -> d o", o=1).unsqueeze(0).to_broadcast([P // D, D, 1]),
                 )
 
-        def load_w(pr):
+        def load_w(c0, c1):
             for g in range(PASSES):
                 nc.sync.dma_start(
-                    out=w_codes[:, g, pr * E:(pr + 1) * E].bitcast(I32),
-                    in_=c_attn_w_words[g].rearrange("p n t -> p (n t)")[:, pr * E * 4:(pr + 1) * E * 4].bitcast(I32),
+                    out=w_codes[:, g, c0:c1].bitcast(I32),
+                    in_=c_attn_w_words[g].rearrange("p n t -> p (n t)")[:, c0 * 4:c1 * 4].bitcast(I32),
                 )
 
         nc.scalar.dma_start(out=b_rows_bf[0:FEATURE_TILES, :], in_=c_attn_b.rearrange("(f p) -> f p", p=P))
         load_conv_constants(nc.scalar, 0)
         for first_tile in range(0, TOKEN_TILES, 2):
             nc.sync.dma_start(out=x_sb[:, first_tile:first_tile + 2, :], in_=x_rows[:, first_tile:first_tile + 2, :])
+        load_w((CONV_ORDER[0] + 1) * GROUP_FEATURES, (CONV_ORDER[0] + 2) * GROUP_FEATURES)
         for quad in range(4):
             nc.sync.dma_start(
                 out=w_planes[32 * quad:32 * quad + 4, :, :].bitcast(I32),
                 in_=c_attn_w_scales[:, 4 * quad:4 * quad + 4, :].rearrange("g r n -> r g n").bitcast(I32),
             )
-        load_w(0)
+        load_w(0, (CONV_ORDER[0] + 1) * GROUP_FEATURES)
         for pr in range(PROJ):
             nc.sync.dma_start(out=b_plain[:, pr, :], in_=c_attn_b[pr * E:pr * E + GROUP_FEATURES].partition_broadcast(P))
         load_conv_constants(nc.sync, 1)
-        load_w(1)
+        load_w(E, 2 * E)
         load_conv_constants(nc.sync, 2)
-        load_w(2)
+        load_w(2 * E, 3 * E)
 
         nc.vector.tensor_copy(out=b_rows[:], in_=b_rows_bf[:])
         b_cols = x_banks.tile([P, S], F32, tag="x")
@@ -154,8 +161,6 @@ def tile_tranceptionblockattention_pa_kernel(
             )
 
         prepare_constants(0)
-        prepare_constants(1)
-        prepare_constants(2)
 
         x_words = x_sb[:].bitcast(F32)
         grouped_words = grouped[:].bitcast(F32)
@@ -182,12 +187,18 @@ def tile_tranceptionblockattention_pa_kernel(
                 )
 
         rounds = [(pr, b, gi) for pr in range(PROJ) for b in range(B) for gi in CONV_ORDER]
+        groups = [(pr, b) for pr in range(PROJ) for b in range(B)]
         tiles = []
         for pr in range(PROJ):
             for b in range(B):
                 for gi in CONV_ORDER:
                     for half in range(HALVES):
                         tiles.append(("conv", pr, b, gi, half))
+                    if gi == CONV_ORDER[0]:
+                        here = groups.index((pr, b))
+                        for ahead in groups[max(here, 1) if here > 0 else 0:here + 2][(1 if here > 0 else 0):]:
+                            for half in range(HALVES):
+                                tiles.append(("slow", ahead[0], ahead[1], SLOW, half))
                 for pair in range(J // 2):
                     tiles.append(("plain", pr, b, pair, 0))
         n_tiles = len(tiles)
@@ -195,6 +206,7 @@ def tile_tranceptionblockattention_pa_kernel(
         acc_of = {}
         split_of = {}
         y_of = {}
+        slow_of = {}
 
         def round_of(t):
             kind, pr, b, gi, half = tiles[t]
@@ -240,6 +252,30 @@ def tile_tranceptionblockattention_pa_kernel(
         def head(t):
             kind, pr, b, gi, half = tiles[t]
             if kind == "plain":
+                return
+            if kind == "slow":
+                xs = xs_ring[groups.index((pr, b)) % SLOW_ROUNDS]
+                nc.scalar.activation(
+                    out=xs[:, half, PAD:PAD + S], in_=bank_of[t][:], func=IDENTITY,
+                    bias=b_attn[:, pr, gi + 1, half:half + 1], scale=1.0,
+                )
+                if half < HALVES - 1:
+                    return
+                early = slow.tile([P, HALVES, S], F32, tag="early")
+                middle = slow.tile([P, HALVES, S], F32, tag="middle")
+                newest = slow.tile([P, HALVES, S], F32, tag="newest")
+                nc.gpsimd.tensor_scalar(
+                    out=early[:], in0=xs[:, :, PAD - 2:PAD - 2 + S], scalar1=tap(pr, gi, 2),
+                    scalar2=cst[pr][:, 3 + gi, 0:1], op0=MULT, op1=ADD,
+                )
+                nc.gpsimd.tensor_scalar(
+                    out=middle[:], in0=xs[:, :, PAD - 1:PAD - 1 + S], scalar1=tap(pr, gi, 1), scalar2=0.0, op0=MULT, op1=ADD,
+                )
+                nc.gpsimd.tensor_tensor(out=early[:], in0=early[:], in1=middle[:], op=ADD)
+                nc.gpsimd.tensor_scalar(
+                    out=newest[:], in0=xs[:, :, PAD:PAD + S], scalar1=tap(pr, gi, 0), scalar2=0.0, op0=MULT, op1=ADD,
+                )
+                slow_of[(pr, b)] = (early, newest)
                 return
             r = round_of(t)
             taps = CONV_TAPS[gi]
@@ -314,6 +350,16 @@ def tile_tranceptionblockattention_pa_kernel(
 
         def turn(t):
             kind, pr, b, gi, half = tiles[t]
+            if kind == "slow":
+                y_slow = y_banks.tile([P, J, P], F32, tag="y")
+                for j in range(J):
+                    for i in range(2):
+                        nc.tensor.matmul(
+                            y_slow[:, j, :], lhsT=slow_of[(pr, b)][i][:, half, j * P:(j + 1) * P], rhs=ident[:],
+                            is_transpose=True, start=(i == 0), stop=(i == 1),
+                        )
+                y_of[t] = y_slow
+                return
             taps = CONV_TAPS[gi]
             n_far = shared_taps(taps)
             far_tile = far_ring[round_of(t) % len(far_ring)]
@@ -338,46 +384,82 @@ def tile_tranceptionblockattention_pa_kernel(
             h0 = (gi + 1) * GROUP_HEADS + half * (P // D)
             y_sb = work.tile([P, P // D, J, D], F32, tag="y_sb")
             nc.scalar.copy(out=y_sb[:], in_=y_of[t][:].rearrange("p j (h d) -> p h j d", d=D))
+            if kind == "slow":
+                nc.sync.dma_start(
+                    out=outs[pr][b, h0:h0 + P // D, :, :].rearrange("h (j p) d -> p (h j) d", p=P),
+                    in_=y_sb[:].rearrange("p h j d -> p (h j) d"),
+                )
+                return
             nc.sync.dma_start(
                 out=outs[pr][b, h0:h0 + P // D, :, :].rearrange("h (p j) d -> p h (j d)", j=J),
                 in_=y_sb[:].rearrange("p h j d -> p h (j d)"),
             )
 
-        for t in range(LOOK):
-            project(t)
-            head(t)
-        state = {"projected": LOOK, "to_store": -1}
+        state = {"projected": 0, "to_store": -1, "banks": 0, "returned": 0}
+        vector_tiles = [t for t in range(n_tiles) if tiles[t][0] != "slow"]
         waiting = [0, 1]
         lanes = [[], []]
 
+        def project_next():
+            state["banks"] = state["banks"] + 1 + state["returned"]
+            state["returned"] = 0
+            while state["banks"] > 0 and state["projected"] < n_tiles:
+                new = state["projected"]
+                state["projected"] = new + 1
+                state["banks"] = state["banks"] - 1
+                project(new)
+                started.append(new)
+                if tiles[new][0] == "slow":
+                    state["returned"] = state["returned"] + 1
+
         def take(lane):
-            t = waiting[lane]
-            if t < n_tiles:
-                waiting[lane] = t + 2
+            i = waiting[lane]
+            if i < len(vector_tiles):
+                waiting[lane] = i + 2
+                t = vector_tiles[i]
                 lanes[lane] = [t] + list(reversed(vector_steps(t)))
+
+        started = []
+        to_store = []
 
         def advance(lane):
             t = lanes[lane][0]
+            kind, pr, b, gi, half = tiles[t]
             vector_step(t, lanes[lane][-1])
             lanes[lane] = lanes[lane][:-1]
             if len(lanes[lane]) > 1:
                 return
             lanes[lane] = []
-            new = state["projected"]
-            if new < n_tiles:
-                project(new)
-            if tiles[t][0] == "conv":
-                turn(t)
-            if state["to_store"] >= 0:
-                store(state["to_store"])
-                state["to_store"] = -1
-            if tiles[t][0] == "conv":
-                state["to_store"] = t
-            if new < n_tiles:
+            project_next()
+            turned = []
+            first_group = (pr, b) == groups[0]
+            if kind == "conv":
+                turned.append(t)
+                if gi == CONV_ORDER[0] and not first_group:
+                    turned.append(tiles.index(("slow", pr, b, SLOW, half)))
+            elif first_group:
+                turned.append(tiles.index(("slow", pr, b, SLOW, gi)))
+            for u in turned:
+                turn(u)
+            for u in to_store:
+                store(u)
+            to_store.clear()
+            to_store.extend(turned)
+            for new in started:
                 head(new)
-                state["projected"] = new + 1
+            started.clear()
             take(lane)
 
+        state["banks"] = LOOK - 1
+        for i in range(2):
+            project_next()
+            state["banks"] = state["banks"] - 1
+            for new in started:
+                head(new)
+            started.clear()
+        state["banks"] = 0
+        prepare_constants(1)
+        prepare_constants(2)
         take(0)
         for i in range((len(lanes[0]) - 1) // 2):
             advance(0)
@@ -387,5 +469,5 @@ def tile_tranceptionblockattention_pa_kernel(
             if lanes[lane]:
                 advance(lane)
             lane = 1 - lane
-        if state["to_store"] >= 0:
-            store(state["to_store"])
+        for u in to_store:
+            store(u)

@@ -92,8 +92,8 @@ def tile_tranceptionblockattention_pa_kernel(
 
         x_rows = hidden_states.flatten_outer_dims().rearrange("(t p) k -> p t k", p=P)
 
-        def load_conv_constants(queue, pr):
-            for gi in range(3):
+        def load_conv_constants(queue, pr, which):
+            for gi in which:
                 taps = CONV_TAPS[gi]
                 queue.dma_start(
                     out=cst_bf[pr][:, gi, LAST - taps:LAST],
@@ -112,7 +112,7 @@ def tile_tranceptionblockattention_pa_kernel(
                 )
 
         nc.scalar.dma_start(out=b_rows_bf[0:FEATURE_TILES, :], in_=c_attn_b.rearrange("(f p) -> f p", p=P))
-        load_conv_constants(nc.scalar, 0)
+        load_conv_constants(nc.scalar, 0, CONV_ORDER)
         for first_tile in range(0, TOKEN_TILES, 2):
             nc.sync.dma_start(out=x_sb[:, first_tile:first_tile + 2, :], in_=x_rows[:, first_tile:first_tile + 2, :])
         load_w((CONV_ORDER[0] + 1) * GROUP_FEATURES, (CONV_ORDER[0] + 2) * GROUP_FEATURES)
@@ -121,46 +121,56 @@ def tile_tranceptionblockattention_pa_kernel(
                 out=w_planes[32 * quad:32 * quad + 4, :, :].bitcast(I32),
                 in_=c_attn_w_scales[:, 4 * quad:4 * quad + 4, :].rearrange("g r n -> r g n").bitcast(I32),
             )
+        load_conv_constants(nc.sync, 0, (SLOW,))
         load_w(0, (CONV_ORDER[0] + 1) * GROUP_FEATURES)
         for pr in range(PROJ):
             nc.sync.dma_start(out=b_plain[:, pr, :], in_=c_attn_b[pr * E:pr * E + GROUP_FEATURES].partition_broadcast(P))
-        load_conv_constants(nc.sync, 1)
+        load_conv_constants(nc.sync, 1, (2, 1, 0))
         load_w(E, 2 * E)
-        load_conv_constants(nc.sync, 2)
+        load_conv_constants(nc.sync, 2, (2, 1, 0))
         load_w(2 * E, 3 * E)
 
-        nc.vector.tensor_copy(out=b_rows[:], in_=b_rows_bf[:])
-        b_cols = x_banks.tile([P, S], F32, tag="x")
-        nc.tensor.transpose(b_cols[:, 0:P], b_rows[:], ident[:])
-        nc.vector.tensor_copy(out=b_attn[:].rearrange("p r g t -> p (r g t)"), in_=b_cols[:, 0:FEATURE_TILES])
+        def spread_bias():
+            nc.vector.tensor_copy(out=b_rows[:], in_=b_rows_bf[:])
+            b_cols = x_banks.tile([P, S], F32, tag="x")
+            nc.tensor.transpose(b_cols[:, 0:P], b_rows[:], ident[:])
+            nc.vector.tensor_copy(out=b_attn[:].rearrange("p r g t -> p (r g t)"), in_=b_cols[:, 0:FEATURE_TILES])
 
         def tap(pr, gi, back):
             return cst[pr][:, gi, LAST - 1 - back:LAST - back]
 
         def prepare_constants(pr):
-            shape = [P, 3, HALVES, LAST]
-            b_here = b_attn[:, pr, 1:4, :].unsqueeze(3).to_broadcast(shape)
-            nc.gpsimd.tensor_copy(out=cst[pr][:], in_=cst_bf[pr][:])
-            nc.gpsimd.tensor_copy(out=csum[pr][:, :, 0:1], in_=cst[pr][:, 0:3, LAST - 1:LAST])
-            for s in range(1, LAST):
+            n_sums = max(CONV_TAPS[gi] - shared_taps(CONV_TAPS[gi]) for gi in CONV_ORDER)
+            sums_shape = [P, 2, HALVES, n_sums]
+            taps_shape = [P, 2, HALVES, LAST]
+            nc.gpsimd.tensor_copy(
+                out=cst[pr][:].rearrange("p (a g) c -> p a g c", a=2)[:, :, 1:3, :],
+                in_=cst_bf[pr][:].rearrange("p (a g) c -> p a g c", a=2)[:, :, 1:3, :],
+            )
+            nc.gpsimd.tensor_copy(out=csum[pr][:, 1:3, 0:1], in_=cst[pr][:, 1:3, LAST - 1:LAST])
+            for s in range(1, n_sums):
                 nc.gpsimd.tensor_tensor(
-                    out=csum[pr][:, :, s:s + 1],
-                    in0=csum[pr][:, :, s - 1:s],
-                    in1=cst[pr][:, 0:3, LAST - 1 - s:LAST - s],
+                    out=csum[pr][:, 1:3, s:s + 1],
+                    in0=csum[pr][:, 1:3, s - 1:s],
+                    in1=cst[pr][:, 1:3, LAST - 1 - s:LAST - s],
                     op=ADD,
                 )
             nc.gpsimd.tensor_tensor(
-                out=bias[pr][:], in0=csum[pr][:].unsqueeze(2).to_broadcast(shape), in1=b_here, op=MULT,
+                out=bias[pr][:, 1:3, :, 0:n_sums], in0=csum[pr][:, 1:3, 0:n_sums].unsqueeze(2).to_broadcast(sums_shape),
+                in1=b_attn[:, pr, 2:4, :].unsqueeze(3).to_broadcast(sums_shape), op=MULT,
             )
             nc.gpsimd.tensor_tensor(
-                out=bias[pr][:], in0=bias[pr][:],
-                in1=cst[pr][:, 3:6, 0:1].unsqueeze(2).to_broadcast(shape), op=ADD,
+                out=bias[pr][:, 1:3, :, 0:n_sums], in0=bias[pr][:, 1:3, :, 0:n_sums],
+                in1=cst[pr][:, 4:6, 0:1].unsqueeze(2).to_broadcast(sums_shape), op=ADD,
             )
             nc.gpsimd.tensor_tensor(
-                out=tap_bias[pr][:], in0=cst[pr][:, 0:3, 0:LAST].unsqueeze(2).to_broadcast(shape), in1=b_here, op=MULT,
+                out=tap_bias[pr][:, 1:3], in0=cst[pr][:, 1:3, 0:LAST].unsqueeze(2).to_broadcast(taps_shape),
+                in1=b_attn[:, pr, 2:4, :].unsqueeze(3).to_broadcast(taps_shape), op=MULT,
             )
-
-        prepare_constants(0)
+            nc.gpsimd.tensor_copy(
+                out=cst[pr][:].rearrange("p (a g) c -> p a g c", a=2)[:, :, 0:1, :],
+                in_=cst_bf[pr][:].rearrange("p (a g) c -> p a g c", a=2)[:, :, 0:1, :],
+            )
 
         x_words = x_sb[:].bitcast(F32)
         grouped_words = grouped[:].bitcast(F32)
@@ -179,6 +189,9 @@ def tile_tranceptionblockattention_pa_kernel(
                     out=grouped_words[:, :, tt * P:(tt + 1) * P, :],
                     in_=xt[:].rearrange("p g u t -> p g t u"),
                 )
+                if tt == 1:
+                    spread_bias()
+                    prepare_constants(0)
             for g in range(PASSES):
                 nc.vector.quantize_mx(
                     out=x_codes[:, g, b * S:(b + 1) * S].bitcast(FP8X4),

@@ -62,9 +62,9 @@ def tile_tranceptionblockattention_pa_kernel(
 
         ident = keep.tile([P, P], F32)
         x_sb = keep.tile([P, TOKEN_TILES, E], BF16)
-        grouped = keep.tile([P, PASSES, B * S, 4], BF16, align_bytes=64)
-        x_codes = keep.tile([P, PASSES, B * S], U32, align_bytes=64)
-        x_planes = keep.tile([P, PASSES, B * S], U8, align_bytes=64)
+        grouped = keep.tile([P, B, PASSES, S, 4], BF16, align_bytes=64)
+        x_codes = keep.tile([P, B, PASSES, S], U32, align_bytes=64)
+        x_planes = keep.tile([P, B, PASSES, S], U8, align_bytes=64)
         w_codes = keep.tile([P, PASSES, PROJ * E], U32, align_bytes=64)
         w_planes = keep.tile([P, PASSES, PROJ * E], U8, align_bytes=64)
         b_rows_bf = keep.tile([P, P], BF16)
@@ -111,20 +111,24 @@ def tile_tranceptionblockattention_pa_kernel(
                     in_=c_attn_w_words[g].rearrange("p n t -> p (n t)")[:, c0 * 4:c1 * 4].bitcast(I32),
                 )
 
+        def load_planes(c0, c1):
+            for quad in range(4):
+                nc.sync.dma_start(
+                    out=w_planes[32 * quad:32 * quad + 4, :, c0:c1].bitcast(I32),
+                    in_=c_attn_w_scales[:, 4 * quad:4 * quad + 4, c0:c1].rearrange("g r n -> r g n").bitcast(I32),
+                )
+
         nc.scalar.dma_start(out=b_rows_bf[0:FEATURE_TILES, :], in_=c_attn_b.rearrange("(f p) -> f p", p=P))
         load_conv_constants(nc.scalar, 0, CONV_ORDER)
         for first_tile in range(0, TOKEN_TILES, 2):
             nc.sync.dma_start(out=x_sb[:, first_tile:first_tile + 2, :], in_=x_rows[:, first_tile:first_tile + 2, :])
         load_w((CONV_ORDER[0] + 1) * GROUP_FEATURES, (CONV_ORDER[0] + 2) * GROUP_FEATURES)
-        for quad in range(4):
-            nc.sync.dma_start(
-                out=w_planes[32 * quad:32 * quad + 4, :, :].bitcast(I32),
-                in_=c_attn_w_scales[:, 4 * quad:4 * quad + 4, :].rearrange("g r n -> r g n").bitcast(I32),
-            )
+        load_planes(0, E)
         load_conv_constants(nc.sync, 0, (SLOW,))
         load_w(0, (CONV_ORDER[0] + 1) * GROUP_FEATURES)
         for pr in range(PROJ):
             nc.sync.dma_start(out=b_plain[:, pr, :], in_=c_attn_b[pr * E:pr * E + GROUP_FEATURES].partition_broadcast(P))
+        load_planes(E, PROJ * E)
         load_conv_constants(nc.sync, 1, (2, 1, 0))
         load_w(E, 2 * E)
         load_conv_constants(nc.sync, 2, (2, 1, 0))
@@ -186,18 +190,17 @@ def tile_tranceptionblockattention_pa_kernel(
                         )
                 copy = nc.vector.tensor_copy if tt % 2 == 0 else nc.scalar.copy
                 copy(
-                    out=grouped_words[:, :, tt * P:(tt + 1) * P, :],
+                    out=grouped_words[:, b, :, (tt - b * J) * P:(tt - b * J + 1) * P, :],
                     in_=xt[:].rearrange("p g u t -> p g t u"),
                 )
                 if tt == 1:
                     spread_bias()
                     prepare_constants(0)
-            for g in range(PASSES):
-                nc.vector.quantize_mx(
-                    out=x_codes[:, g, b * S:(b + 1) * S].bitcast(FP8X4),
-                    scales=x_planes[:, g, b * S:(b + 1) * S],
-                    in_=grouped[:, g, b * S:(b + 1) * S, :].rearrange("p t c -> p (t c)"),
-                )
+            nc.vector.quantize_mx(
+                out=x_codes[:, b].rearrange("p g t -> p (g t)").bitcast(FP8X4),
+                scales=x_planes[:, b].rearrange("p g t -> p (g t)"),
+                in_=grouped[:, b].rearrange("p g t c -> p (g t c)"),
+            )
 
         rounds = [(pr, b, gi) for pr in range(PROJ) for b in range(B) for gi in CONV_ORDER]
         groups = [(pr, b) for pr in range(PROJ) for b in range(B)]
@@ -235,12 +238,12 @@ def tile_tranceptionblockattention_pa_kernel(
                 cols = slice(pr * E, pr * E + GROUP_FEATURES)
                 z_ps = x_banks.tile([P, 2, GROUP_FEATURES], F32, tag="x")
                 for i in range(2):
-                    tokens = slice((b * J + 2 * pair + i) * P, (b * J + 2 * pair + i + 1) * P)
+                    tokens = slice((2 * pair + i) * P, (2 * pair + i + 1) * P)
                     for g in range(PASSES):
                         nc.tensor.matmul_mx(
                             out=z_ps[:, i, :],
-                            lhsT=x_codes[:, g, tokens].bitcast(FP8X4),
-                            lhsT_scale=x_planes[:, g, tokens],
+                            lhsT=x_codes[:, b, g, tokens].bitcast(FP8X4),
+                            lhsT_scale=x_planes[:, b, g, tokens],
                             rhs=w_codes[:, g, cols].bitcast(FP8X4),
                             rhs_scale=w_planes[:, g, cols],
                             start=(g == 0),
@@ -255,8 +258,8 @@ def tile_tranceptionblockattention_pa_kernel(
                     out=x_ps[:],
                     lhsT=w_codes[:, g, c0:c0 + P].bitcast(FP8X4),
                     lhsT_scale=w_planes[:, g, c0:c0 + P],
-                    rhs=x_codes[:, g, b * S:(b + 1) * S].bitcast(FP8X4),
-                    rhs_scale=x_planes[:, g, b * S:(b + 1) * S],
+                    rhs=x_codes[:, b, g, :].bitcast(FP8X4),
+                    rhs_scale=x_planes[:, b, g, :],
                     start=(g == 0),
                     stop=(g == PASSES - 1),
                 )

@@ -111,6 +111,9 @@ def tile_tranceptionblockattention_pa_kernel(
                     in_=c_attn_w_words[g].rearrange("p n t -> p (n t)")[:, c0 * 4:c1 * 4].bitcast(I32),
                 )
 
+        def load_plain_bias(pr):
+            nc.sync.dma_start(out=b_plain[:, pr, :], in_=c_attn_b[pr * E:pr * E + GROUP_FEATURES].partition_broadcast(P))
+
         def load_planes(c0, c1):
             for quad in range(4):
                 nc.sync.dma_start(
@@ -126,13 +129,14 @@ def tile_tranceptionblockattention_pa_kernel(
         load_planes(0, E)
         load_conv_constants(nc.sync, 0, (SLOW,))
         load_w(0, (CONV_ORDER[0] + 1) * GROUP_FEATURES)
-        for pr in range(PROJ):
-            nc.sync.dma_start(out=b_plain[:, pr, :], in_=c_attn_b[pr * E:pr * E + GROUP_FEATURES].partition_broadcast(P))
+        load_plain_bias(0)
         load_planes(E, PROJ * E)
         load_conv_constants(nc.sync, 1, (2, 1, 0))
         load_w(E, 2 * E)
+        load_plain_bias(1)
         load_conv_constants(nc.sync, 2, (2, 1, 0))
         load_w(2 * E, 3 * E)
+        load_plain_bias(2)
 
         def spread_bias():
             nc.vector.tensor_copy(out=b_rows[:], in_=b_rows_bf[:])

@@ -76,7 +76,8 @@ def tile_tranceptionblockattention_pa_kernel(
         csum = [keep.tile([P, 3, LAST], F32, name="csum%d" % pr) for pr in range(PROJ)]
         bias = [keep.tile([P, 3, HALVES, LAST], F32, name="bias%d" % pr) for pr in range(PROJ)]
         tap_bias = [keep.tile([P, 3, HALVES, LAST], F32, name="tap_bias%d" % pr) for pr in range(PROJ)]
-        far_ring = [keep.tile([P, HALVES, MOST_SHARED, J, PAD + P], F32, name="far%d" % i) for i in range(AHEAD + 2)]
+        far_ring = [keep.tile([P, HALVES, MOST_SHARED, PAD + S], F32, name="far%d" % i) for i in range(AHEAD + 2)]
+        far_last = [keep.tile([P, HALVES, MOST_SHARED, J, PAD + P], F32, name="far_last%d" % i) for i in range(len(CONV_ORDER))]
         xs_ring = [keep.tile([P, HALVES, PAD + S], F32, name="xs%d" % i) for i in range(SLOW_ROUNDS)]
 
         nc.vector.memset(cst_bf[0][:], 0.0)
@@ -86,6 +87,8 @@ def tile_tranceptionblockattention_pa_kernel(
         nc.vector.memset(cst_bf[2][:], 0.0)
         make_identity(nc, ident[:])
         for far_tile in far_ring:
+            nc.gpsimd.memset(far_tile[:, :, :, 0:PAD], 0.0)
+        for far_tile in far_last:
             nc.gpsimd.memset(far_tile[:, :, :, :, 0:PAD], 0.0)
         for xs_tile in xs_ring:
             nc.gpsimd.memset(xs_tile[:, :, 0:PAD], 0.0)
@@ -232,6 +235,10 @@ def tile_tranceptionblockattention_pa_kernel(
             kind, pr, b, gi, half = tiles[t]
             return rounds.index((pr, b, gi))
 
+        def long_pieces(t):
+            kind, pr, b, gi, half = tiles[t]
+            return kind == "conv" and (pr, b) == groups[-1]
+
         def by_partition(ap):
             return ap.rearrange("f (p j) -> f p j", j=J)
 
@@ -314,8 +321,9 @@ def tile_tranceptionblockattention_pa_kernel(
             for k in range(shared_taps(taps)):
                 back = first + 1 + k
                 nc.scalar.activation(
-                    out=far_ring[r % len(far_ring)][:, half, k, :, PAD:PAD + P].rearrange("f j p -> f p j"),
-                    in_=by_partition(bank_of[t][:]),
+                    out=(far_last[CONV_ORDER.index(gi)][:, half, k, :, PAD:PAD + P].rearrange("f j p -> f p j")
+                         if long_pieces(t) else far_ring[r % len(far_ring)][:, half, k, PAD:PAD + S]),
+                    in_=by_partition(bank_of[t][:]) if long_pieces(t) else bank_of[t][:],
                     func=IDENTITY,
                     bias=tap_bias[pr][:, gi, half, LAST - 1 - back:LAST - back],
                     scale=tap(pr, gi, back),
@@ -347,7 +355,7 @@ def tile_tranceptionblockattention_pa_kernel(
                     )
                 return
             acc = acc_of[round_of(t)]
-            if back > 0:
+            if back > 0 or not long_pieces(t):
                 nc.vector.scalar_tensor_tensor(
                     out=acc[:, half, back:S],
                     in0=bank_of[t][:, 0:S - back],
@@ -370,19 +378,26 @@ def tile_tranceptionblockattention_pa_kernel(
 
         def turn(t):
             kind, pr, b, gi, half = tiles[t]
-            if kind == "slow":
-                y_slow = y_banks.tile([P, J, P], F32, tag="y")
-                for j in range(J):
-                    for i in range(2):
-                        nc.tensor.matmul(
-                            y_slow[:, j, :], lhsT=slow_of[(pr, b)][i][:, half, j * P:(j + 1) * P], rhs=ident[:],
-                            is_transpose=True, start=(i == 0), stop=(i == 1),
-                        )
-                y_of[t] = y_slow
-                return
             taps = CONV_TAPS[gi]
             n_far = shared_taps(taps)
-            far_tile = far_ring[round_of(t) % len(far_ring)]
+            if not long_pieces(t):
+                if kind == "slow":
+                    terms = [part[:, half, :] for part in slow_of[(pr, b)]]
+                else:
+                    terms = [acc_of[round_of(t)][:, half, :]]
+                    for k in range(n_far):
+                        back = taps - n_far + k
+                        terms.append(far_ring[round_of(t) % len(far_ring)][:, half, k, PAD - back:PAD - back + S])
+                y_nat = y_banks.tile([P, J, P], F32, tag="y")
+                for j in range(J):
+                    for i in range(len(terms)):
+                        nc.tensor.matmul(
+                            y_nat[:, j, :], lhsT=terms[i][:, j * P:(j + 1) * P], rhs=ident[:],
+                            is_transpose=True, start=(i == 0), stop=(i == len(terms) - 1),
+                        )
+                y_of[t] = y_nat
+                return
+            far_tile = far_last[CONV_ORDER.index(gi)]
             y_ps = y_banks.tile([P, J, P], F32, tag="y")
             for j in range(J):
                 nc.tensor.matmul(
@@ -404,7 +419,7 @@ def tile_tranceptionblockattention_pa_kernel(
             h0 = (gi + 1) * GROUP_HEADS + half * (P // D)
             y_sb = work.tile([P, P // D, J, D], F32, tag="y_sb")
             nc.scalar.copy(out=y_sb[:], in_=y_of[t][:].rearrange("p j (h d) -> p h j d", d=D))
-            if kind == "slow":
+            if not long_pieces(t):
                 nc.sync.dma_start(
                     out=outs[pr][b, h0:h0 + P // D, :, :].rearrange("h (j p) d -> p (h j) d", p=P),
                     in_=y_sb[:].rearrange("p h j d -> p (h j) d"),

@@ -31,6 +31,7 @@ SLOW = 0
 SLOW_ROUNDS = 3
 AHEAD = 3
 LOOK = AHEAD * HALVES
+WARM_UP = 5
 MOST_SHARED = 1
 
 FLOPS = 2 * B * S * E * PROJ * E
@@ -61,6 +62,7 @@ def tile_tranceptionblockattention_pa_kernel(
             tc.manual_schedule():
 
         ident = keep.tile([P, P], F32)
+        idle_in = keep.tile([P, S], BF16)
         x_sb = keep.tile([P, TOKEN_TILES, E], BF16)
         grouped = keep.tile([P, B, PASSES, S, 4], BF16, align_bytes=64)
         x_codes = keep.tile([P, B, PASSES, S], U32, align_bytes=64)
@@ -80,6 +82,10 @@ def tile_tranceptionblockattention_pa_kernel(
         far_last = [keep.tile([P, HALVES, MOST_SHARED, J, PAD + P], F32, name="far_last%d" % i) for i in range(len(CONV_ORDER))]
         xs_ring = [keep.tile([P, HALVES, PAD + S], F32, name="xs%d" % i) for i in range(SLOW_ROUNDS)]
 
+        nc.vector.memset(idle_in[:], 0.0)
+        idle_out = y_banks.tile([P, S], F32, tag="y")
+        for i in range(WARM_UP):
+            nc.tensor.matmul(idle_out[:], lhsT=idle_in[:, 0:P], rhs=idle_in[:], start=True, stop=True)
         nc.vector.memset(cst_bf[0][:], 0.0)
         nc.vector.memset(b_rows_bf[:], 0.0)
         nc.vector.memset(w_planes[:].bitcast(I32), 0)

@@ -206,6 +206,8 @@ def tile_tranceptionblockattention_pa_kernel(
                     out=grouped_words[:, b, :, (tt - b * J) * P:(tt - b * J + 1) * P, :],
                     in_=xt[:].rearrange("p g u t -> p g t u"),
                 )
+                if tt % 2 == 1:
+                    nc.tensor.matmul(idle_out[:], lhsT=idle_in[:, 0:P], rhs=idle_in[:], start=True, stop=True)
                 if tt == 1:
                     spread_bias()
                     prepare_constants(0)

@@ -132,7 +132,9 @@ def tile_tranceptionblockattention_pa_kernel(
 
         nc.scalar.dma_start(out=b_rows_bf[0:FEATURE_TILES, :], in_=c_attn_b.rearrange("(f p) -> f p", p=P))
         load_conv_constants(nc.scalar, 0, CONV_ORDER)
-        for first_tile in range(0, TOKEN_TILES, 2):
+        for tt in range(2):
+            nc.sync.dma_start(out=x_sb[:, tt, :], in_=x_rows[:, tt, :])
+        for first_tile in range(2, TOKEN_TILES, 2):
             nc.sync.dma_start(out=x_sb[:, first_tile:first_tile + 2, :], in_=x_rows[:, first_tile:first_tile + 2, :])
         load_w((CONV_ORDER[0] + 1) * GROUP_FEATURES, (CONV_ORDER[0] + 2) * GROUP_FEATURES)
         load_planes(0, E)

import concourse.mybir as mybir
from concourse.masks import make_identity

F32 = mybir.dt.float32
BF16 = mybir.dt.bfloat16
U8 = mybir.dt.uint8
U32 = mybir.dt.uint32
I32 = mybir.dt.int32
FP8X4 = mybir.dt.float8_e4m3fn_x4
MULT = mybir.AluOpType.mult
ADD = mybir.AluOpType.add
IDENTITY = mybir.ActivationFunctionType.Identity

P = 128
B, S, E, H, D = 2, 512, 1024, 16, 64
PROJ = 3
K_PASS = 512
PASSES = E // K_PASS
TOKEN_TILES = B * S // P
CONV_TAPS = (3, 5, 7)
GROUP_FEATURES = E // 4
HALVES = GROUP_FEATURES // P
GROUP_HEADS = GROUP_FEATURES // D
FEATURE_TILES = PROJ * E // P
J = S // P
SLOT = 16
LAST = 9
PAD = 8
CONV_ORDER = (2, 1)
SLOW = 0
SLOW_ROUNDS = 3
AHEAD = 3
LOOK = AHEAD * HALVES
WARM_UP = 5
MOST_SHARED = 1

FLOPS = 2 * B * S * E * PROJ * E


def tile_tranceptionblockattention_pa_kernel(
    tc,
    hidden_states, c_attn_w_words, c_attn_w_scales, c_attn_b,
    qw3, qb3, qw5, qb5, qw7, qb7,
    kw3, kb3, kw5, kb5, kw7, kb7,
    vw3, vb3, vw5, vb5, vw7, vb7,
    out_0, out_1, out_2,
):
    nc = tc.nc
    conv_w = ((qw3, qw5, qw7), (kw3, kw5, kw7), (vw3, vw5, vw7))
    conv_b = ((qb3, qb5, qb7), (kb3, kb5, kb7), (vb3, vb5, vb7))
    outs = (out_0, out_1, out_2)

    def shared_taps(taps):
        return 1

    with tc.tile_pool(name="keep", bufs=1) as keep, \
            tc.tile_pool(name="work", bufs=6) as work, \
            tc.tile_pool(name="sums", bufs=AHEAD + 2) as sums, \
            tc.tile_pool(name="slow", bufs=SLOW_ROUNDS) as slow, \
            tc.psum_pool(name="x_banks", bufs=AHEAD * HALVES) as x_banks, \
            tc.psum_pool(name="y_banks", bufs=HALVES) as y_banks, \
            tc.manual_schedule():

        ident = keep.tile([P, P], F32)
        idle_in = keep.tile([P, S], BF16)
        x_sb = keep.tile([P, TOKEN_TILES, E], BF16)
        grouped = keep.tile([P, B, PASSES, S, 4], BF16, align_bytes=64)
        x_codes = keep.tile([P, B, PASSES, S], U32, align_bytes=64)
        x_planes = keep.tile([P, B, PASSES, S], U8, align_bytes=64)
        w_codes = keep.tile([P, PASSES, PROJ * E], U32, align_bytes=64)
        w_planes = keep.tile([P, PASSES, PROJ * E], U8, align_bytes=64)
        b_rows_bf = keep.tile([P, P], BF16)
        b_rows = keep.tile([P, P], F32)
        b_attn = keep.tile([P, PROJ, 4, HALVES], F32)
        b_plain = keep.tile([P, PROJ, GROUP_FEATURES], BF16)
        cst_bf = [keep.tile([P, 6, SLOT], BF16, name="cst_bf%d" % pr) for pr in range(PROJ)]
        cst = [keep.tile([P, 6, SLOT], F32, name="cst%d" % pr) for pr in range(PROJ)]
        csum = [keep.tile([P, 3, LAST], F32, name="csum%d" % pr) for pr in range(PROJ)]
        bias = [keep.tile([P, 3, HALVES, LAST], F32, name="bias%d" % pr) for pr in range(PROJ)]
        tap_bias = [keep.tile([P, 3, HALVES, LAST], F32, name="tap_bias%d" % pr) for pr in range(PROJ)]
        far_ring = [keep.tile([P, HALVES, MOST_SHARED, PAD + S], F32, name="far%d" % i) for i in range(AHEAD + 2)]
        far_last = [keep.tile([P, HALVES, MOST_SHARED, J, PAD + P], F32, name="far_last%d" % i) for i in range(len(CONV_ORDER))]
        xs_ring = [keep.tile([P, HALVES, PAD + S], F32, name="xs%d" % i) for i in range(SLOW_ROUNDS)]

        nc.vector.memset(idle_in[:], 0.0)
        idle_out = y_banks.tile([P, S], F32, tag="y")
        for i in range(WARM_UP):
            nc.tensor.matmul(idle_out[:], lhsT=idle_in[:, 0:P], rhs=idle_in[:], start=True, stop=True)
        nc.vector.memset(cst_bf[0][:], 0.0)
        nc.vector.memset(b_rows_bf[:], 0.0)
        nc.vector.memset(w_planes[:].bitcast(I32), 0)
        nc.vector.memset(cst_bf[1][:], 0.0)
        nc.vector.memset(cst_bf[2][:], 0.0)
        make_identity(nc, ident[:])
        for far_tile in far_ring:
            nc.gpsimd.memset(far_tile[:, :, :, 0:PAD], 0.0)
        for far_tile in far_last:
            nc.gpsimd.memset(far_tile[:, :, :, :, 0:PAD], 0.0)
        for xs_tile in xs_ring:
            nc.gpsimd.memset(xs_tile[:, :, 0:PAD], 0.0)

        x_rows = hidden_states.flatten_outer_dims().rearrange("(t p) k -> p t k", p=P)

        def load_conv_constants(queue, pr, which):
            for gi in which:
                taps = CONV_TAPS[gi]
                queue.dma_start(
                    out=cst_bf[pr][:, gi, LAST - taps:LAST],
                    in_=conv_w[pr][gi].unsqueeze(0).to_broadcast([P // D, D, taps]),
                )
                queue.dma_start(
                    out=cst_bf[pr][:, 3 + gi, 0:1],
                    in_=conv_b[pr][gi].rearrange("(d o) -> d o", o=1).unsqueeze(0).to_broadcast([P // D, D, 1]),
                )

        def load_w(c0, c1):
            for g in range(PASSES):
                nc.sync.dma_start(
                    out=w_codes[:, g, c0:c1].bitcast(I32),
                    in_=c_attn_w_words[g].rearrange("p n t -> p (n t)")[:, c0 * 4:c1 * 4].bitcast(I32),
                )

        def load_plain_bias(pr):
            nc.sync.dma_start(out=b_plain[:, pr, :], in_=c_attn_b[pr * E:pr * E + GROUP_FEATURES].partition_broadcast(P))

        def load_planes(c0, c1):
            for quad in range(4):
                nc.sync.dma_start(
                    out=w_planes[32 * quad:32 * quad + 4, :, c0:c1].bitcast(I32),
                    in_=c_attn_w_scales[:, 4 * quad:4 * quad + 4, c0:c1].rearrange("g r n -> r g n").bitcast(I32),
                )

        nc.scalar.dma_start(out=b_rows_bf[0:FEATURE_TILES, :], in_=c_attn_b.rearrange("(f p) -> f p", p=P))
        load_conv_constants(nc.scalar, 0, CONV_ORDER)
        for tt in range(2):
            nc.sync.dma_start(out=x_sb[:, tt, :], in_=x_rows[:, tt, :])
        for first_tile in range(2, TOKEN_TILES, 2):
            nc.sync.dma_start(out=x_sb[:, first_tile:first_tile + 2, :], in_=x_rows[:, first_tile:first_tile + 2, :])
        load_w((CONV_ORDER[0] + 1) * GROUP_FEATURES, (CONV_ORDER[0] + 2) * GROUP_FEATURES)
        load_planes(0, E)
        load_conv_constants(nc.sync, 0, (SLOW,))
        load_w(0, (CONV_ORDER[0] + 1) * GROUP_FEATURES)
        load_plain_bias(0)
        load_planes(E, PROJ * E)
        load_conv_constants(nc.sync, 1, (2, 1, 0))
        load_w(E, 2 * E)
        load_plain_bias(1)
        load_conv_constants(nc.sync, 2, (2, 1, 0))
        load_w(2 * E, 3 * E)
        load_plain_bias(2)

        def spread_bias():
            nc.vector.tensor_copy(out=b_rows[:], in_=b_rows_bf[:])
            b_cols = x_banks.tile([P, S], F32, tag="x")
            nc.tensor.transpose(b_cols[:, 0:P], b_rows[:], ident[:])
            nc.vector.tensor_copy(out=b_attn[:].rearrange("p r g t -> p (r g t)"), in_=b_cols[:, 0:FEATURE_TILES])

        def tap(pr, gi, back):
            return cst[pr][:, gi, LAST - 1 - back:LAST - back]

        def prepare_constants(pr):
            n_sums = max(CONV_TAPS[gi] - shared_taps(CONV_TAPS[gi]) for gi in CONV_ORDER)
            sums_shape = [P, 2, HALVES, n_sums]
            taps_shape = [P, 2, HALVES, LAST]
            nc.gpsimd.tensor_copy(
                out=cst[pr][:].rearrange("p (a g) c -> p a g c", a=2)[:, :, 1:3, :],
                in_=cst_bf[pr][:].rearrange("p (a g) c -> p a g c", a=2)[:, :, 1:3, :],
            )
            nc.gpsimd.tensor_copy(out=csum[pr][:, 1:3, 0:1], in_=cst[pr][:, 1:3, LAST - 1:LAST])
            for s in range(1, n_sums):
                nc.gpsimd.tensor_tensor(
                    out=csum[pr][:, 1:3, s:s + 1],
                    in0=csum[pr][:, 1:3, s - 1:s],
                    in1=cst[pr][:, 1:3, LAST - 1 - s:LAST - s],
                    op=ADD,
                )
            nc.gpsimd.tensor_tensor(
                out=bias[pr][:, 1:3, :, 0:n_sums], in0=csum[pr][:, 1:3, 0:n_sums].unsqueeze(2).to_broadcast(sums_shape),
                in1=b_attn[:, pr, 2:4, :].unsqueeze(3).to_broadcast(sums_shape), op=MULT,
            )
            nc.gpsimd.tensor_tensor(
                out=bias[pr][:, 1:3, :, 0:n_sums], in0=bias[pr][:, 1:3, :, 0:n_sums],
                in1=cst[pr][:, 4:6, 0:1].unsqueeze(2).to_broadcast(sums_shape), op=ADD,
            )
            nc.gpsimd.tensor_tensor(
                out=tap_bias[pr][:, 1:3], in0=cst[pr][:, 1:3, 0:LAST].unsqueeze(2).to_broadcast(taps_shape),
                in1=b_attn[:, pr, 2:4, :].unsqueeze(3).to_broadcast(taps_shape), op=MULT,
            )
            nc.gpsimd.tensor_copy(
                out=cst[pr][:].rearrange("p (a g) c -> p a g c", a=2)[:, :, 0:1, :],
                in_=cst_bf[pr][:].rearrange("p (a g) c -> p a g c", a=2)[:, :, 0:1, :],
            )

        x_words = x_sb[:].bitcast(F32)
        grouped_words = grouped[:].bitcast(F32)
        for b in range(B):
            for tt in range(b * J, (b + 1) * J):
                xt = x_banks.tile([P, PASSES, 2, P], F32, tag="x")
                for g in range(PASSES):
                    for u in range(2):
                        nc.tensor.transpose(
                            xt[:, g, u, :],
                            x_words[:, tt, 256 * g + u:256 * (g + 1):2],
                            ident[:],
                        )
                copy = nc.vector.tensor_copy if tt % 2 == 0 else nc.scalar.copy
                copy(
                    out=grouped_words[:, b, :, (tt - b * J) * P:(tt - b * J + 1) * P, :],
                    in_=xt[:].rearrange("p g u t -> p g t u"),
                )
                if tt % 2 == 1:
                    nc.tensor.matmul(idle_out[:], lhsT=idle_in[:, 0:P], rhs=idle_in[:], start=True, stop=True)
                if tt == 1:
                    spread_bias()
                    prepare_constants(0)
            nc.vector.quantize_mx(
                out=x_codes[:, b].rearrange("p g t -> p (g t)").bitcast(FP8X4),
                scales=x_planes[:, b].rearrange("p g t -> p (g t)"),
                in_=grouped[:, b].rearrange("p g t c -> p (g t c)"),
            )

        rounds = [(pr, b, gi) for pr in range(PROJ) for b in range(B) for gi in CONV_ORDER]
        groups = [(pr, b) for pr in range(PROJ) for b in range(B)]
        tiles = []
        for pr in range(PROJ):
            for b in range(B):
                for gi in CONV_ORDER:
                    for half in range(HALVES):
                        tiles.append(("conv", pr, b, gi, half))
                    if gi == CONV_ORDER[0]:
                        here = groups.index((pr, b))
                        for ahead in groups[max(here, 1) if here > 0 else 0:here + 2][(1 if here > 0 else 0):]:
                            for half in range(HALVES):
                                tiles.append(("slow", ahead[0], ahead[1], SLOW, half))
                for pair in range(J // 2):
                    tiles.append(("plain", pr, b, pair, 0))
        n_tiles = len(tiles)
        bank_of = {}
        acc_of = {}
        split_of = {}
        y_of = {}
        slow_of = {}

        def round_of(t):
            kind, pr, b, gi, half = tiles[t]
            return rounds.index((pr, b, gi))

        def long_pieces(t):
            kind, pr, b, gi, half = tiles[t]
            return kind == "conv" and (pr, b) == groups[-1]

        def by_partition(ap):
            return ap.rearrange("f (p j) -> f p j", j=J)

        def project(t):
            kind, pr, b, gi, half = tiles[t]
            if kind == "plain":
                pair = gi
                cols = slice(pr * E, pr * E + GROUP_FEATURES)
                z_ps = x_banks.tile([P, 2, GROUP_FEATURES], F32, tag="x")
                for i in range(2):
                    tokens = slice((2 * pair + i) * P, (2 * pair + i + 1) * P)
                    for g in range(PASSES):
                        nc.tensor.matmul_mx(
                            out=z_ps[:, i, :],
                            lhsT=x_codes[:, b, g, tokens].bitcast(FP8X4),
                            lhsT_scale=x_planes[:, b, g, tokens],
                            rhs=w_codes[:, g, cols].bitcast(FP8X4),
                            rhs_scale=w_planes[:, g, cols],
                            start=(g == 0),
                            stop=(g == PASSES - 1),
                        )
                bank_of[t] = z_ps
                return
            c0 = pr * E + (gi + 1) * GROUP_FEATURES + half * P
            x_ps = x_banks.tile([P, S], F32, tag="x")
            for g in range(PASSES):
                nc.tensor.matmul_mx(
                    out=x_ps[:],
                    lhsT=w_codes[:, g, c0:c0 + P].bitcast(FP8X4),
                    lhsT_scale=w_planes[:, g, c0:c0 + P],
                    rhs=x_codes[:, b, g, :].bitcast(FP8X4),
                    rhs_scale=x_planes[:, b, g, :],
                    start=(g == 0),
                    stop=(g == PASSES - 1),
                )
            bank_of[t] = x_ps

        def head(t):
            kind, pr, b, gi, half = tiles[t]
            if kind == "plain":
                return
            if kind == "slow":
                xs = xs_ring[groups.index((pr, b)) % SLOW_ROUNDS]
                nc.scalar.activation(
                    out=xs[:, half, PAD:PAD + S], in_=bank_of[t][:], func=IDENTITY,
                    bias=b_attn[:, pr, gi + 1, half:half + 1], scale=1.0,
                )
                if half < HALVES - 1:
                    return
                early = slow.tile([P, HALVES, S], F32, tag="early")
                middle = slow.tile([P, HALVES, S], F32, tag="middle")
                newest = slow.tile([P, HALVES, S], F32, tag="newest")
                nc.gpsimd.tensor_scalar(
                    out=early[:], in0=xs[:, :, PAD - 2:PAD - 2 + S], scalar1=tap(pr, gi, 2),
                    scalar2=cst[pr][:, 3 + gi, 0:1], op0=MULT, op1=ADD,
                )
                nc.gpsimd.tensor_scalar(
                    out=middle[:], in0=xs[:, :, PAD - 1:PAD - 1 + S], scalar1=tap(pr, gi, 1), scalar2=0.0, op0=MULT, op1=ADD,
                )
                nc.gpsimd.tensor_tensor(out=early[:], in0=early[:], in1=middle[:], op=ADD)
                nc.gpsimd.tensor_scalar(
                    out=newest[:], in0=xs[:, :, PAD:PAD + S], scalar1=tap(pr, gi, 0), scalar2=0.0, op0=MULT, op1=ADD,
                )
                slow_of[(pr, b)] = (early, newest)
                return
            r = round_of(t)
            taps = CONV_TAPS[gi]
            first = taps - 1 - shared_taps(taps)
            if half == 0:
                acc = sums.tile([P, HALVES, S], F32, tag="acc")
                acc_of[r] = acc
                nc.scalar.copy(out=acc[:, :, 0:first], in_=bias[pr][:, gi, :, 0:first])
            nc.scalar.activation(
                out=acc_of[r][:, half, first:S],
                in_=bank_of[t][:, 0:S - first],
                func=IDENTITY,
                bias=bias[pr][:, gi, half, first:first + 1],
                scale=tap(pr, gi, first),
            )
            for k in range(shared_taps(taps)):
                back = first + 1 + k
                nc.scalar.activation(
                    out=(far_last[CONV_ORDER.index(gi)][:, half, k, :, PAD:PAD + P].rearrange("f j p -> f p j")
                         if long_pieces(t) else far_ring[r % len(far_ring)][:, half, k, PAD:PAD + S]),
                    in_=by_partition(bank_of[t][:]) if long_pieces(t) else bank_of[t][:],
                    func=IDENTITY,
                    bias=tap_bias[pr][:, gi, half, LAST - 1 - back:LAST - back],
                    scale=tap(pr, gi, back),
                )

        def vector_steps(t):
            kind, pr, b, gi, half = tiles[t]
            if kind == "plain":
                return [0]
            taps = CONV_TAPS[gi]
            return list(range(taps - 2 - shared_taps(taps), -1, -1))

        def vector_step(t, back):
            kind, pr, b, gi, half = tiles[t]
            if kind == "plain":
                pair = gi
                z_sb = work.tile([P, 2, GROUP_FEATURES], F32, tag="z_sb")
                nc.vector.tensor_tensor(
                    out=z_sb[:],
                    in0=bank_of[t][:],
                    in1=b_plain[:, pr, :].unsqueeze(1).to_broadcast([P, 2, GROUP_FEATURES]),
                    op=ADD,
                )
                for i in range(2):
                    s0 = (2 * pair + i) * P
                    nc.sync.dma_start(
                        out=outs[pr][b, 0:GROUP_HEADS, s0:s0 + P, :].rearrange("h p d -> p h d"),
                        in_=z_sb[:, i, :].rearrange("p (h d) -> p h d", d=D),
                    )
                return
            acc = acc_of[round_of(t)]
            if back > 0 or not long_pieces(t):
                nc.vector.scalar_tensor_tensor(
                    out=acc[:, half, back:S],
                    in0=bank_of[t][:, 0:S - back],
                    scalar=tap(pr, gi, back),
                    in1=acc[:, half, back:S],
                    op0=MULT,
                    op1=ADD,
                )
            else:
                split = work.tile([P, J, P], F32, tag="split")
                split_of[t] = split
                nc.vector.scalar_tensor_tensor(
                    out=split[:].rearrange("f j p -> f p j"),
                    in0=by_partition(bank_of[t][:]),
                    scalar=tap(pr, gi, 0),
                    in1=by_partition(acc[:, half, :]),
                    op0=MULT,
                    op1=ADD,
                )

        def turn(t):
            kind, pr, b, gi, half = tiles[t]
            taps = CONV_TAPS[gi]
            n_far = shared_taps(taps)
            if not long_pieces(t):
                if kind == "slow":
                    terms = [part[:, half, :] for part in slow_of[(pr, b)]]
                else:
                    terms = [acc_of[round_of(t)][:, half, :]]
                    for k in range(n_far):
                        back = taps - n_far + k
                        terms.append(far_ring[round_of(t) % len(far_ring)][:, half, k, PAD - back:PAD - back + S])
                y_nat = y_banks.tile([P, J, P], F32, tag="y")
                for j in range(J):
                    for i in range(len(terms)):
                        nc.tensor.matmul(
                            y_nat[:, j, :], lhsT=terms[i][:, j * P:(j + 1) * P], rhs=ident[:],
                            is_transpose=True, start=(i == 0), stop=(i == len(terms) - 1),
                        )
                y_of[t] = y_nat
                return
            far_tile = far_last[CONV_ORDER.index(gi)]
            y_ps = y_banks.tile([P, J, P], F32, tag="y")
            for j in range(J):
                nc.tensor.matmul(
                    y_ps[:, j, :], lhsT=split_of[t][:, j, :], rhs=ident[:],
                    is_transpose=True, start=True, stop=(n_far == 0),
                )
                for k in range(n_far):
                    back = taps - n_far + k
                    j_far = (j - back) % J
                    carry = (back - j + j_far) // J
                    nc.tensor.matmul(
                        y_ps[:, j, :], lhsT=far_tile[:, half, k, j_far, PAD - carry:PAD - carry + P], rhs=ident[:],
                        is_transpose=True, start=False, stop=(k == n_far - 1),
                    )
            y_of[t] = y_ps

        def store(t):
            kind, pr, b, gi, half = tiles[t]
            h0 = (gi + 1) * GROUP_HEADS + half * (P // D)
            y_sb = work.tile([P, P // D, J, D], F32, tag="y_sb")
            nc.scalar.copy(out=y_sb[:], in_=y_of[t][:].rearrange("p j (h d) -> p h j d", d=D))
            if not long_pieces(t):
                nc.sync.dma_start(
                    out=outs[pr][b, h0:h0 + P // D, :, :].rearrange("h (j p) d -> p (h j) d", p=P),
                    in_=y_sb[:].rearrange("p h j d -> p (h j) d"),
                )
                return
            nc.sync.dma_start(
                out=outs[pr][b, h0:h0 + P // D, :, :].rearrange("h (p j) d -> p h (j d)", j=J),
                in_=y_sb[:].rearrange("p h j d -> p h (j d)"),
            )

        state = {"projected": 0, "to_store": -1, "banks": 0, "returned": 0}
        vector_tiles = [t for t in range(n_tiles) if tiles[t][0] != "slow"]
        waiting = [0, 1]
        lanes = [[], []]

        def project_next():
            state["banks"] = state["banks"] + 1 + state["returned"]
            state["returned"] = 0
            while state["banks"] > 0 and state["projected"] < n_tiles:
                new = state["projected"]
                state["projected"] = new + 1
                state["banks"] = state["banks"] - 1
                project(new)
                started.append(new)
                if tiles[new][0] == "slow":
                    state["returned"] = state["returned"] + 1

        def take(lane):
            i = waiting[lane]
            if i < len(vector_tiles):
                waiting[lane] = i + 2
                t = vector_tiles[i]
                lanes[lane] = [t] + list(reversed(vector_steps(t)))

        started = []
        to_store = []

        def advance(lane):
            t = lanes[lane][0]
            kind, pr, b, gi, half = tiles[t]
            vector_step(t, lanes[lane][-1])
            lanes[lane] = lanes[lane][:-1]
            if len(lanes[lane]) > 1:
                return
            lanes[lane] = []
            project_next()
            turned = []
            first_group = (pr, b) == groups[0]
            if kind == "conv":
                turned.append(t)
                if gi == CONV_ORDER[0] and not first_group:
                    turned.append(tiles.index(("slow", pr, b, SLOW, half)))
            elif first_group:
                turned.append(tiles.index(("slow", pr, b, SLOW, gi)))
            for u in turned:
                turn(u)
            for u in to_store:
                store(u)
            to_store.clear()
            to_store.extend(turned)
            for new in started:
                head(new)
            started.clear()
            take(lane)

        state["banks"] = LOOK - 1
        for i in range(2):
            project_next()
            state["banks"] = state["banks"] - 1
            for new in started:
                head(new)
            started.clear()
        state["banks"] = 0
        prepare_constants(1)
        prepare_constants(2)
        take(0)
        for i in range((len(lanes[0]) - 1) // 2):
            advance(0)
        take(1)
        lane = 1
        while lanes[0] or lanes[1]:
            if lanes[lane]:
                advance(lane)
            lane = 1 - lane
        for u in to_store:
            store(u)
